import numpy as np
import ml_dtypes


def mxq(x, axis, fmt="e4m3"):
    dtype, down = {"e4m3": (ml_dtypes.float8_e4m3fn, 7), "e5m2": (ml_dtypes.float8_e5m2, 14)}[fmt]
    v = np.moveaxis(np.asarray(x, np.float32).astype(ml_dtypes.bfloat16).astype(np.float64), axis, -1)
    blocks = v.reshape(v.shape[:-1] + (-1, 32))
    amax = np.abs(blocks).max(-1, keepdims=True)
    byte = np.maximum(np.where(amax > 0, np.frexp(amax)[1] - 1 + 127, 0) - down, 1)
    scale = np.exp2(byte - 127.0)
    codes = (blocks / scale).astype(np.float32).astype(dtype).astype(np.float64)
    return np.moveaxis((codes * scale).reshape(v.shape), -1, axis)


WIDE = False


def mx_kscale(k):
    if not WIDE:
        return np.ones(k)
    levels = np.array([10, -10, 5, -5, 0])
    a = np.random.permutation(np.resize(levels, k // 512 * 4)).reshape(k // 512, 4)
    idx = np.arange(k)
    return np.exp2(a[idx // 512, idx % 128 // 32])


BF16 = ml_dtypes.bfloat16


def bf(x):
    return np.asarray(x, np.float32).astype(BF16)


def f64(x):
    return np.asarray(x).astype(np.float64)


E2M1 = np.array([0.0, 0.5, 1.0, 1.5, 2.0, 3.0, 4.0, 6.0, -0.0, -0.5, -1.0, -1.5, -2.0, -3.0, -4.0, -6.0])


def pack_weight(w, fmt):
    k, n = w.shape
    w = f64(bf(w)).reshape(k // 32, 32, n)
    amax = np.abs(w).max(1)
    if fmt == "e4m3":
        byte = np.frexp(amax)[1] - 1 + 127 - 7
    else:
        mant, ex = np.frexp(amax / 6.0)
        byte = np.where(mant > 0.5, ex, ex - 1) + 127
    byte = np.clip(np.where(amax > 0, byte, 1), 1, 254)
    scaled = (w * np.exp2(127.0 - byte)[:, None, :]).reshape(k, n).astype(np.float32)
    by_word = np.ascontiguousarray(scaled.reshape(k // 512, 128, 4, n).transpose(0, 1, 3, 2))
    if fmt == "e4m3":
        words = by_word.astype(ml_dtypes.float8_e4m3fn).view(np.uint8)
    else:
        c = by_word.astype(ml_dtypes.float4_e2m1fn).view(np.uint8) & 0xF
        words = c[..., 0::2] | (c[..., 1::2] << 4)
    return np.ascontiguousarray(words), np.ascontiguousarray(byte.astype(np.uint8).reshape(k // 512, 16, n))


def unpack_weight(words, scales, fmt):
    g, p, n, _ = words.shape
    if fmt == "e4m3":
        vals = np.ascontiguousarray(words).view(ml_dtypes.float8_e4m3fn).astype(np.float64)
    else:
        nib = np.empty((g, p, n, 4), np.uint8)
        nib[..., 0::2] = words & 0xF
        nib[..., 1::2] = words >> 4
        vals = E2M1[nib]
    vals = vals * np.repeat(np.exp2(scales.astype(np.float64) - 127.0), 8, axis=1)[..., None]
    return vals.transpose(0, 1, 3, 2).reshape(g * 512, n)


B, S, D, H, DN, DR, DV, RQ, RKV = 2, 256, 2048, 16, 64, 128, 128, 1536, 512
THETA = 10000.0
EPS = 1e-6


def rmsnorm(v, w):
    return v * (1.0 / np.sqrt(np.mean(v * v, axis=-1, keepdims=True) + EPS)) * w


def rotate_half(v):
    v1 = v[..., ::2]
    v2 = v[..., 1::2]
    return np.stack((-v2, v1), axis=-1).reshape(v.shape)


def rope_cache():
    inv_freq = 1.0 / THETA ** (np.arange(0, DR, 2) / DR)
    freqs = np.outer(np.arange(S), inv_freq)
    emb = np.concatenate((freqs, freqs), -1)
    return np.cos(emb), np.sin(emb)


def apply_rope(v, cos, sin):
    return v * cos[None, None] + rotate_half(v) * sin[None, None]


def setup_inputs():
    s, t = mx_kscale(D), mx_kscale(RKV)
    x = bf(np.random.standard_normal((B, S, D)) * s)
    Wkva_words, Wkva_scales = pack_weight(np.random.standard_normal((D, RKV + DR)) / np.sqrt(D) / s[:, None], "e4m3")
    kv_a_norm_w = bf((1.0 + 0.1 * np.random.standard_normal(RKV)) * t)
    Wkvb_words, Wkvb_scales = pack_weight(np.random.standard_normal((RKV, H * (DN + DV))) / np.sqrt(RKV) / t[:, None], "e4m3")
    return {"x": x,
            "Wkva_words": Wkva_words,
            "Wkva_scales": Wkva_scales,
            "kv_a_norm_w": kv_a_norm_w,
            "Wkvb_words": Wkvb_words,
            "Wkvb_scales": Wkvb_scales}


def reference(x, Wkva_words, Wkva_scales, kv_a_norm_w, Wkvb_words, Wkvb_scales):
    kv_a = mxq(f64(x), 2, "e4m3") @ unpack_weight(Wkva_words, Wkva_scales, "e4m3")
    kv_latent, k_rope_shared = kv_a[..., :RKV], kv_a[..., RKV:]
    h = rmsnorm(kv_latent, f64(kv_a_norm_w))
    kv = mxq(h, 2, "e4m3") @ unpack_weight(Wkvb_words, Wkvb_scales, "e4m3")
    kv = kv.reshape(B, S, H, DN + DV).transpose(0, 2, 1, 3)
    k_nope, v = kv[..., :DN], kv[..., DN:]
    cos, sin = rope_cache()
    k_rope = apply_rope(k_rope_shared[:, None], cos, sin)
    k_rope = np.broadcast_to(k_rope, (B, H, S, DR))
    k_final = np.concatenate([k_nope, k_rope], -1)
    return k_final, v

@@ -1,0 +1,302 @@
+import math
+from contextlib import ExitStack
+
+import concourse.mybir as mybir
+from concourse.masks import make_identity
+
+F32 = mybir.dt.float32
+BF16 = mybir.dt.bfloat16
+I32 = mybir.dt.int32
+U32 = mybir.dt.uint32
+U8 = mybir.dt.uint8
+FP8X4 = mybir.dt.float8_e4m3fn_x4
+ALU = mybir.AluOpType
+ACT = mybir.ActivationFunctionType
+
+P = 128
+PACK = 4
+K_PASS = P * PACK
+
+BATCH, SEQ, D_MODEL = 2, 256, 2048
+LATENT, ROPE = 512, 128
+HEADS, NOPE, VDIM = 16, 64, 128
+A_COLS = LATENT + ROPE
+HEAD_COLS = NOPE + VDIM
+B_COLS = HEADS * HEAD_COLS
+K_OUT = NOPE + ROPE
+THETA = 10000.0
+EPS = 1e-6
+
+GROUPS = D_MODEL // K_PASS
+TOK = SEQ // P
+PAIR = 2
+PAIR_COLS = PAIR * HEAD_COLS
+N_PAIRS = HEADS // PAIR
+QUADS = 4
+PLANES = 4
+B_PLANE_COLS = B_COLS // PLANES
+
+ROUND_MAGIC = 1.5 * 2.0**23
+
+FLOPS = 2 * BATCH * SEQ * (D_MODEL * A_COLS + LATENT * B_COLS)
+
+
+def tile_multiheadlatentattention_pb_kernel(
+    tc, x, Wkva_words, Wkva_scales, kv_a_norm_w, Wkvb_words, Wkvb_scales, out_0, out_1
+):
+    nc = tc.nc
+    with ExitStack() as ctx:
+        const = ctx.enter_context(tc.tile_pool(name="const", bufs=1))
+        xin = ctx.enter_context(tc.tile_pool(name="xin", bufs=BATCH))
+        xq = ctx.enter_context(tc.tile_pool(name="xq", bufs=BATCH * TOK))
+        norm = ctx.enter_context(tc.tile_pool(name="norm", bufs=BATCH * TOK))
+        rope = ctx.enter_context(tc.tile_pool(name="rope", bufs=BATCH))
+        outs = ctx.enter_context(tc.tile_pool(name="outs", bufs=BATCH))
+        tp_ps = ctx.enter_context(tc.psum_pool(name="tp_ps", bufs=2))
+        lat_ps = ctx.enter_context(tc.psum_pool(name="lat_ps", bufs=TOK))
+        rope_ps = ctx.enter_context(tc.psum_pool(name="rope_ps", bufs=1))
+        kv_ps = ctx.enter_context(tc.psum_pool(name="kv_ps", bufs=3))
+
+        wa_planes = const.tile([P, A_COLS], U8, align_bytes=64)
+        wb_planes = const.tile([P, B_PLANE_COLS], U8, align_bytes=64)
+        nc.vector.memset(wa_planes[:].bitcast(I32), 0)
+        nc.vector.memset(wb_planes[:].bitcast(I32), 0)
+
+        wa_words = const.tile([P, GROUPS, A_COLS], U32, align_bytes=64)
+        wb_words = const.tile([P, B_COLS], U32, align_bytes=64)
+        gain_bf = const.tile([P, PACK], BF16)
+        x_sb = []
+        for b in range(BATCH):
+            x_b = xin.tile([P, TOK, D_MODEL], BF16, name="x_b")
+            x_sb.append(x_b)
+
+        def load_x(b):
+            for j in range(TOK):
+                nc.sync.dma_start(
+                    out=x_sb[b][:, j, :],
+                    in_=x[b].rearrange("(p j) k -> p j k", j=TOK)[:, j, :],
+                )
+
+        for quad in range(QUADS):
+            nc.sync.dma_start(
+                out=wa_planes[32 * quad : 32 * quad + 16, :].bitcast(I32),
+                in_=Wkva_scales[:, 4 * quad : 4 * quad + 4, :].bitcast(I32),
+            )
+        load_x(0)
+        for g in range(GROUPS):
+            nc.sync.dma_start(
+                out=wa_words[:, g, :].bitcast(I32),
+                in_=Wkva_words[g].rearrange("p n t -> p (n t)").bitcast(I32),
+            )
+        for quad in range(QUADS):
+            nc.sync.dma_start(
+                out=wb_planes[32 * quad : 32 * quad + 16, :].bitcast(I32),
+                in_=Wkvb_scales[0, 4 * quad : 4 * quad + 4, :]
+                .rearrange("r (c n) -> c r n", c=PLANES)
+                .bitcast(I32),
+            )
+        nc.sync.dma_start(out=gain_bf[:], in_=kv_a_norm_w.rearrange("(p t) -> p t", t=PACK))
+        wb_dram = Wkvb_words[0].rearrange("p n t -> p (n t)").bitcast(I32)
+        for c in range(PLANES):
+            cols = slice(c * B_PLANE_COLS, (c + 1) * B_PLANE_COLS)
+            nc.sync.dma_start(out=wb_words[:, cols].bitcast(I32), in_=wb_dram[:, cols])
+        load_x(1)
+
+        ident = const.tile([P, P], F32)
+        make_identity(nc, ident[:])
+        gain = const.tile([P, PACK], F32)
+        nc.vector.tensor_copy(out=gain[:], in_=gain_bf[:])
+
+        freq = const.tile([P, ROPE], F32)
+        nc.vector.memset(freq[:, 0:1], 1.0)
+        for step in range(6):
+            n = 2**step
+            nc.vector.tensor_scalar(
+                out=freq[:, n : 2 * n], in0=freq[:, 0:n],
+                scalar1=math.pow(THETA, -n / 64.0), scalar2=None, op0=ALU.mult,
+            )
+        nc.vector.tensor_copy(out=freq[:, 64:128], in_=freq[:, 0:64])
+        carried = const.tile([P, ROPE // 2, 2], F32)
+        freq_pairs = freq[:].rearrange("p (m e) -> p m e", e=2)
+        nc.vector.tensor_copy(out=carried[:, :, 0], in_=freq_pairs[:, :, 1])
+        nc.vector.tensor_scalar(
+            out=carried[:, :, 1], in0=freq_pairs[:, :, 0], scalar1=-1.0, scalar2=None, op0=ALU.mult
+        )
+        position = const.tile([P, TOK], I32)
+        nc.gpsimd.iota(position[:], pattern=[[1, TOK]], base=0, channel_multiplier=TOK)
+        turns = const.tile([P, TOK], F32)
+        nc.vector.tensor_scalar(
+            out=turns[:], in0=position[:], scalar1=1.0 / (2.0 * math.pi), scalar2=None, op0=ALU.mult
+        )
+        angle = const.tile([P, 2, TOK, ROPE], F32)
+        for j in range(TOK):
+            nc.vector.tensor_scalar(
+                out=angle[:, 0, j, :], in0=freq[:],
+                scalar1=turns[:, j : j + 1], scalar2=0.25, op0=ALU.mult, op1=ALU.add,
+            )
+            nc.vector.tensor_scalar(
+                out=angle[:, 1, j, :], in0=carried[:].rearrange("p m e -> p (m e)"),
+                scalar1=turns[:, j : j + 1], scalar2=None, op0=ALU.mult,
+            )
+        angle_flat = angle[:].rearrange("p c j f -> p (c j f)")
+        shifted = const.tile([P, 2 * TOK * ROPE], F32)
+        nc.vector.tensor_scalar(
+            out=shifted[:], in0=angle_flat, scalar1=ROUND_MAGIC, scalar2=None, op0=ALU.add
+        )
+        minus_frac = const.tile([P, 2 * TOK * ROPE], F32)
+        nc.vector.scalar_tensor_tensor(
+            out=minus_frac[:], in0=shifted[:], scalar=ROUND_MAGIC, in1=angle_flat,
+            op0=ALU.subtract, op1=ALU.subtract,
+        )
+        tab = const.tile([P, 2, TOK * ROPE], F32)
+        nc.scalar.activation(
+            out=tab[:].rearrange("p c f -> p (c f)"), in_=minus_frac[:], func=ACT.Sin,
+            scale=-2.0 * math.pi,
+        )
+        warm = const.tile([P, 1], F32)
+        nc.scalar.activation(out=warm[:], in_=tab[:, 0, 0:1], func=ACT.Sqrt, bias=1.0, scale=0.0)
+
+        def quantise_x(b, j):
+            x_words = x_sb[b][:].bitcast(F32)
+            grouped = xq.tile([P, GROUPS, P, PACK], BF16, align_bytes=64)
+            grouped_words = grouped[:].bitcast(F32)
+            for half in range(GROUPS // 2):
+                xt = tp_ps.tile([P, 2, 2, P], F32, tag="tp")
+                for gi in range(2):
+                    g = 2 * half + gi
+                    for u in range(2):
+                        nc.tensor.transpose(
+                            out=xt[:, gi, u, :],
+                            in_=x_words[:, j, 256 * g + u : 256 * (g + 1) : 2],
+                            identity=ident[:],
+                        )
+                copy = nc.vector.tensor_copy if half == 0 else nc.scalar.copy
+                copy(
+                    out=grouped_words[:, 2 * half : 2 * half + 2, :, :],
+                    in_=xt[:].rearrange("p g u k -> p g k u"),
+                )
+            codes = xq.tile([P, GROUPS * P], U32, align_bytes=64)
+            scales = xq.tile([P, GROUPS * P], U8, align_bytes=64)
+            nc.vector.quantize_mx(
+                out=codes[:].bitcast(FP8X4),
+                scales=scales[:],
+                in_=grouped[:].rearrange("p g k t -> p (g k t)"),
+            )
+            return codes, scales
+
+        def first_pass(x_mx_j, g, n_cols, acc):
+            codes, scales = x_mx_j
+            nc.tensor.matmul_mx(
+                out=acc,
+                lhsT=codes[:, g * P : (g + 1) * P].bitcast(FP8X4),
+                lhsT_scale=scales[:, g * P : (g + 1) * P],
+                rhs=wa_words[:, g, n_cols].bitcast(FP8X4),
+                rhs_scale=wa_planes[4 * g : P, n_cols],
+                start=(g == 0),
+                stop=(g == GROUPS - 1),
+            )
+
+        def quantise_h(latent):
+            squares = norm.tile([P, LATENT], BF16)
+            mean_sq = norm.tile([P, 1], F32)
+            nc.scalar.activation(
+                out=squares[:], in_=latent[:], func=ACT.Square,
+                scale=1.0 / math.sqrt(LATENT), accum_out=mean_sq[:],
+            )
+            rms = norm.tile([P, 1], F32)
+            nc.scalar.activation(out=rms[:], in_=mean_sq[:], func=ACT.Sqrt, bias=EPS, scale=1.0)
+            rstd = norm.tile([P, 1], F32)
+            nc.vector.reciprocal(out=rstd[:], in_=rms[:])
+            normed = norm.tile([P, PACK, P], F32)
+            nc.vector.tensor_scalar(
+                out=normed[:], in0=latent[:].rearrange("p (q t) -> p t q", t=PACK),
+                scalar1=rstd[:, 0:1], scalar2=None, op0=ALU.mult,
+            )
+            normed_t = tp_ps.tile([P, PACK, P], F32, tag="tp")
+            for t in range(PACK):
+                nc.tensor.transpose(out=normed_t[:, t, :], in_=normed[:, t, :], identity=ident[:])
+            h_grouped = norm.tile([P, P, PACK], BF16, align_bytes=64)
+            nc.vector.tensor_tensor(
+                out=h_grouped[:], in0=normed_t[:].rearrange("p t k -> p k t"),
+                in1=gain[:].unsqueeze(1).to_broadcast([P, P, PACK]), op=ALU.mult,
+            )
+            codes = norm.tile([P, P], U32, align_bytes=64)
+            scales = norm.tile([P, P], U8, align_bytes=64)
+            nc.vector.quantize_mx(
+                out=codes[:].bitcast(FP8X4),
+                scales=scales[:],
+                in_=h_grouped[:].rearrange("p k t -> p (k t)"),
+            )
+            return codes, scales
+
+        def rotate(r_bank, k_sb):
+            prod = rope.tile([P, 2, TOK * ROPE], F32)
+            nc.vector.tensor_tensor(
+                out=prod[:], in0=r_bank.unsqueeze(1).to_broadcast([P, 2, TOK * ROPE]),
+                in1=tab[:], op=ALU.mult,
+            )
+            own = prod[:, 0, :].rearrange("p (m e) -> p m e", e=2)
+            carry = prod[:, 1, :].rearrange("p (m e) -> p m e", e=2)
+            rotated = rope.tile([P, TOK, ROPE], F32)
+            rotated_pairs = rotated[:].rearrange("p j (m e) -> p (j m) e", e=2)
+            for e in range(2):
+                nc.vector.tensor_tensor(
+                    out=rotated_pairs[:, :, e], in0=own[:, :, e], in1=carry[:, :, 1 - e], op=ALU.add
+                )
+            for pair in range(N_PAIRS):
+                heads = slice(PAIR * pair, PAIR * (pair + 1))
+                nc.gpsimd.tensor_scalar(
+                    out=k_sb[:, heads, :, NOPE:K_OUT],
+                    in0=rotated[:].unsqueeze(1).to_broadcast([P, PAIR, TOK, ROPE]),
+                    scalar1=1.0, scalar2=0.0, op0=ALU.mult, op1=ALU.add,
+                )
+
+        def second_matmul(b, h_mx, k_sb, v_sb):
+            for pair in range(N_PAIRS):
+                heads = slice(PAIR * pair, PAIR * (pair + 1))
+                plane = (pair * PAIR_COLS) // B_PLANE_COLS
+                in_plane = (pair * PAIR_COLS) % B_PLANE_COLS
+                for j in range(TOK):
+                    codes, scales = h_mx[j]
+                    kv = kv_ps.tile([P, 512], F32)
+                    for lo, hi in ((0, 256), (256, PAIR_COLS)):
+                        nc.tensor.matmul_mx(
+                            out=kv[:, lo:hi],
+                            lhsT=codes[:].bitcast(FP8X4),
+                            lhsT_scale=scales[:],
+                            rhs=wb_words[:, pair * PAIR_COLS + lo : pair * PAIR_COLS + hi].bitcast(FP8X4),
+                            rhs_scale=wb_planes[4 * plane : P, in_plane + lo : in_plane + hi],
+                            start=True,
+                            stop=True,
+                        )
+                    by_head = kv[:, 0:PAIR_COLS].rearrange("p (h c) -> p h c", h=PAIR)
+                    copy = nc.vector.tensor_copy if j == 0 else nc.scalar.copy
+                    copy(out=k_sb[:, heads, j, 0:NOPE], in_=by_head[:, :, 0:NOPE])
+                    copy(out=v_sb[:, heads, j, :], in_=by_head[:, :, NOPE:HEAD_COLS])
+                nc.sync.dma_start(
+                    out=out_0[b, heads].rearrange("h (p j) d -> p h (j d)", j=TOK),
+                    in_=k_sb[:, heads, :, :].rearrange("p h j d -> p h (j d)"),
+                )
+                nc.sync.dma_start(
+                    out=out_1[b, heads].rearrange("h (p j) d -> p h (j d)", j=TOK),
+                    in_=v_sb[:, heads, :, :].rearrange("p h j d -> p h (j d)"),
+                )
+
+        for b in range(BATCH):
+            x_mx = [quantise_x(b, j) for j in range(TOK)]
+            latent = []
+            for j in range(TOK):
+                latent_j = lat_ps.tile([P, LATENT], F32, name="latent_j")
+                latent.append(latent_j)
+            for g in range(GROUPS):
+                for j in range(TOK):
+                    first_pass(x_mx[j], g, slice(0, LATENT), latent[j][:])
+            r_bank = rope_ps.tile([P, 512], F32)
+            for j in range(TOK):
+                for g in range(GROUPS):
+                    first_pass(x_mx[j], g, slice(LATENT, A_COLS), r_bank[:, j * ROPE : (j + 1) * ROPE])
+            h_mx = [quantise_h(latent[j]) for j in range(TOK)]
+            k_sb = outs.tile([P, HEADS, TOK, K_OUT], F32)
+            v_sb = outs.tile([P, HEADS, TOK, VDIM], F32)
+            rotate(r_bank[:, 0 : TOK * ROPE], k_sb)
+            second_matmul(b, h_mx, k_sb, v_sb)

@@ -82,12 +82,14 @@ def tile_multiheadlatentattention_pb_kernel(
                 out=wa_planes[32 * quad : 32 * quad + 16, :].bitcast(I32),
                 in_=Wkva_scales[:, 4 * quad : 4 * quad + 4, :].bitcast(I32),
             )
+        nc.sync.dma_start(out=gain_bf[:], in_=kv_a_norm_w.rearrange("(p t) -> p t", t=PACK))
         load_x(0)
         for g in range(GROUPS):
             nc.sync.dma_start(
                 out=wa_words[:, g, :].bitcast(I32),
                 in_=Wkva_words[g].rearrange("p n t -> p (n t)").bitcast(I32),
             )
+        load_x(1)
         for quad in range(QUADS):
             nc.sync.dma_start(
                 out=wb_planes[32 * quad : 32 * quad + 16, :].bitcast(I32),
@@ -95,12 +97,10 @@ def tile_multiheadlatentattention_pb_kernel(
                 .rearrange("r (c n) -> c r n", c=PLANES)
                 .bitcast(I32),
             )
-        nc.sync.dma_start(out=gain_bf[:], in_=kv_a_norm_w.rearrange("(p t) -> p t", t=PACK))
         wb_dram = Wkvb_words[0].rearrange("p n t -> p (n t)").bitcast(I32)
         for c in range(PLANES):
             cols = slice(c * B_PLANE_COLS, (c + 1) * B_PLANE_COLS)
             nc.sync.dma_start(out=wb_words[:, cols].bitcast(I32), in_=wb_dram[:, cols])
-        load_x(1)
 
         ident = const.tile([P, P], F32)
         make_identity(nc, ident[:])
@@ -282,21 +282,24 @@ def tile_multiheadlatentattention_pb_kernel(
                     in_=v_sb[:, heads, :, :].rearrange("p h j d -> p h (j d)"),
                 )
 
+        h_mx, k_sb, v_sb = [], [], []
         for b in range(BATCH):
             x_mx = [quantise_x(b, j) for j in range(TOK)]
             latent = []
             for j in range(TOK):
                 latent_j = lat_ps.tile([P, LATENT], F32, name="latent_j")
                 latent.append(latent_j)
-            for g in range(GROUPS):
-                for j in range(TOK):
-                    first_pass(x_mx[j], g, slice(0, LATENT), latent[j][:])
+                for g in range(GROUPS):
+                    first_pass(x_mx[j], g, slice(0, LATENT), latent_j[:])
             r_bank = rope_ps.tile([P, 512], F32)
             for j in range(TOK):
                 for g in range(GROUPS):
                     first_pass(x_mx[j], g, slice(LATENT, A_COLS), r_bank[:, j * ROPE : (j + 1) * ROPE])
-            h_mx = [quantise_h(latent[j]) for j in range(TOK)]
-            k_sb = outs.tile([P, HEADS, TOK, K_OUT], F32)
-            v_sb = outs.tile([P, HEADS, TOK, VDIM], F32)
-            rotate(r_bank[:, 0 : TOK * ROPE], k_sb)
-            second_matmul(b, h_mx, k_sb, v_sb)
+            h_mx.append([quantise_h(latent[j]) for j in range(TOK)])
+            k_b = outs.tile([P, HEADS, TOK, K_OUT], F32, name="k_b")
+            v_b = outs.tile([P, HEADS, TOK, VDIM], F32, name="v_b")
+            k_sb.append(k_b)
+            v_sb.append(v_b)
+            rotate(r_bank[:, 0 : TOK * ROPE], k_b)
+        for b in range(BATCH):
+            second_matmul(b, h_mx[b], k_sb[b], v_sb[b])

@@ -36,6 +36,9 @@ QUADS = 4
 PLANES = 4
 B_PLANE_COLS = B_COLS // PLANES
 
+EARLY_ROPE = 1
+NOPE_STORE_PAIRS = 4
+
 ROUND_MAGIC = 1.5 * 2.0**23
 
 FLOPS = 2 * BATCH * SEQ * (D_MODEL * A_COLS + LATENT * B_COLS)
@@ -82,14 +85,12 @@ def tile_multiheadlatentattention_pb_kernel(
                 out=wa_planes[32 * quad : 32 * quad + 16, :].bitcast(I32),
                 in_=Wkva_scales[:, 4 * quad : 4 * quad + 4, :].bitcast(I32),
             )
-        nc.sync.dma_start(out=gain_bf[:], in_=kv_a_norm_w.rearrange("(p t) -> p t", t=PACK))
         load_x(0)
         for g in range(GROUPS):
             nc.sync.dma_start(
                 out=wa_words[:, g, :].bitcast(I32),
                 in_=Wkva_words[g].rearrange("p n t -> p (n t)").bitcast(I32),
             )
-        load_x(1)
         for quad in range(QUADS):
             nc.sync.dma_start(
                 out=wb_planes[32 * quad : 32 * quad + 16, :].bitcast(I32),
@@ -97,10 +98,12 @@ def tile_multiheadlatentattention_pb_kernel(
                 .rearrange("r (c n) -> c r n", c=PLANES)
                 .bitcast(I32),
             )
+        nc.sync.dma_start(out=gain_bf[:], in_=kv_a_norm_w.rearrange("(p t) -> p t", t=PACK))
         wb_dram = Wkvb_words[0].rearrange("p n t -> p (n t)").bitcast(I32)
         for c in range(PLANES):
             cols = slice(c * B_PLANE_COLS, (c + 1) * B_PLANE_COLS)
             nc.sync.dma_start(out=wb_words[:, cols].bitcast(I32), in_=wb_dram[:, cols])
+        load_x(1)
 
         ident = const.tile([P, P], F32)
         make_identity(nc, ident[:])
@@ -229,7 +232,7 @@ def tile_multiheadlatentattention_pb_kernel(
             )
             return codes, scales
 
-        def rotate(r_bank, k_sb):
+        def rotate(r_bank):
             prod = rope.tile([P, 2, TOK * ROPE], F32)
             nc.vector.tensor_tensor(
                 out=prod[:], in0=r_bank.unsqueeze(1).to_broadcast([P, 2, TOK * ROPE]),
@@ -243,10 +246,20 @@ def tile_multiheadlatentattention_pb_kernel(
                 nc.vector.tensor_tensor(
                     out=rotated_pairs[:, :, e], in0=own[:, :, e], in1=carry[:, :, 1 - e], op=ALU.add
                 )
+            return rotated
+
+        def store_rope(b, rotated):
+            for j in range(TOK):
+                nc.sync.dma_start(
+                    out=out_0[b].rearrange("h (p j) d -> p h j d", j=TOK)[:, :, j, NOPE:K_OUT],
+                    in_=rotated[:, j, :].unsqueeze(1).to_broadcast([P, HEADS, ROPE]),
+                )
+
+        def spread_rope(rotated, k_rows):
             for pair in range(N_PAIRS):
                 heads = slice(PAIR * pair, PAIR * (pair + 1))
                 nc.gpsimd.tensor_scalar(
-                    out=k_sb[:, heads, :, NOPE:K_OUT],
+                    out=k_rows[:, heads, :, NOPE:K_OUT],
                     in0=rotated[:].unsqueeze(1).to_broadcast([P, PAIR, TOK, ROPE]),
                     scalar1=1.0, scalar2=0.0, op0=ALU.mult, op1=ALU.add,
                 )
@@ -273,33 +286,43 @@ def tile_multiheadlatentattention_pb_kernel(
                     copy = nc.vector.tensor_copy if j == 0 else nc.scalar.copy
                     copy(out=k_sb[:, heads, j, 0:NOPE], in_=by_head[:, :, 0:NOPE])
                     copy(out=v_sb[:, heads, j, :], in_=by_head[:, :, NOPE:HEAD_COLS])
-                nc.sync.dma_start(
-                    out=out_0[b, heads].rearrange("h (p j) d -> p h (j d)", j=TOK),
-                    in_=k_sb[:, heads, :, :].rearrange("p h j d -> p h (j d)"),
-                )
+                if b >= EARLY_ROPE:
+                    nc.sync.dma_start(
+                        out=out_0[b, heads].rearrange("h (p j) d -> p h (j d)", j=TOK),
+                        in_=k_sb[:, heads, :, :].rearrange("p h j d -> p h (j d)"),
+                    )
+                elif pair % NOPE_STORE_PAIRS == NOPE_STORE_PAIRS - 1:
+                    done = slice(PAIR * (pair + 1 - NOPE_STORE_PAIRS), PAIR * (pair + 1))
+                    for j in range(TOK):
+                        nc.sync.dma_start(
+                            out=out_0[b, done].rearrange("h (p j) d -> p h j d", j=TOK)[:, :, j, 0:NOPE],
+                            in_=k_sb[:, done, j, :],
+                        )
                 nc.sync.dma_start(
                     out=out_1[b, heads].rearrange("h (p j) d -> p h (j d)", j=TOK),
                     in_=v_sb[:, heads, :, :].rearrange("p h j d -> p h (j d)"),
                 )
 
-        h_mx, k_sb, v_sb = [], [], []
         for b in range(BATCH):
             x_mx = [quantise_x(b, j) for j in range(TOK)]
             latent = []
             for j in range(TOK):
                 latent_j = lat_ps.tile([P, LATENT], F32, name="latent_j")
                 latent.append(latent_j)
-                for g in range(GROUPS):
-                    first_pass(x_mx[j], g, slice(0, LATENT), latent_j[:])
+            for g in range(GROUPS):
+                for j in range(TOK):
+                    first_pass(x_mx[j], g, slice(0, LATENT), latent[j][:])
             r_bank = rope_ps.tile([P, 512], F32)
             for j in range(TOK):
                 for g in range(GROUPS):
                     first_pass(x_mx[j], g, slice(LATENT, A_COLS), r_bank[:, j * ROPE : (j + 1) * ROPE])
-            h_mx.append([quantise_h(latent[j]) for j in range(TOK)])
-            k_b = outs.tile([P, HEADS, TOK, K_OUT], F32, name="k_b")
-            v_b = outs.tile([P, HEADS, TOK, VDIM], F32, name="v_b")
-            k_sb.append(k_b)
-            v_sb.append(v_b)
-            rotate(r_bank[:, 0 : TOK * ROPE], k_b)
-        for b in range(BATCH):
-            second_matmul(b, h_mx[b], k_sb[b], v_sb[b])
+            h_mx = [quantise_h(latent[j]) for j in range(TOK)]
+            rotated = rotate(r_bank[:, 0 : TOK * ROPE])
+            if b < EARLY_ROPE:
+                store_rope(b, rotated)
+                k_sb = outs.tile([P, HEADS, TOK, NOPE], F32, name="k_nope_sb", bufs=1)
+            else:
+                k_sb = outs.tile([P, HEADS, TOK, K_OUT], F32, name="k_sb", bufs=1)
+                spread_rope(rotated, k_sb)
+            v_sb = outs.tile([P, HEADS, TOK, VDIM], F32)
+            second_matmul(b, h_mx, k_sb, v_sb)

@@ -36,9 +36,6 @@ QUADS = 4
 PLANES = 4
 B_PLANE_COLS = B_COLS // PLANES
 
-EARLY_ROPE = 1
-NOPE_STORE_PAIRS = 4
-
 ROUND_MAGIC = 1.5 * 2.0**23
 
 FLOPS = 2 * BATCH * SEQ * (D_MODEL * A_COLS + LATENT * B_COLS)
@@ -62,8 +59,8 @@ def tile_multiheadlatentattention_pb_kernel(
 
         wa_planes = const.tile([P, A_COLS], U8, align_bytes=64)
         wb_planes = const.tile([P, B_PLANE_COLS], U8, align_bytes=64)
-        nc.vector.memset(wa_planes[:].bitcast(I32), 0)
-        nc.vector.memset(wb_planes[:].bitcast(I32), 0)
+        nc.gpsimd.memset(wa_planes[:].bitcast(F32), 0.0)
+        nc.gpsimd.memset(wb_planes[:].bitcast(F32), 0.0)
 
         wa_words = const.tile([P, GROUPS, A_COLS], U32, align_bytes=64)
         wb_words = const.tile([P, B_COLS], U32, align_bytes=64)
@@ -73,37 +70,39 @@ def tile_multiheadlatentattention_pb_kernel(
             x_b = xin.tile([P, TOK, D_MODEL], BF16, name="x_b")
             x_sb.append(x_b)
 
-        def load_x(b):
-            for j in range(TOK):
-                nc.sync.dma_start(
-                    out=x_sb[b][:, j, :],
-                    in_=x[b].rearrange("(p j) k -> p j k", j=TOK)[:, j, :],
-                )
+        def load_x(b, j):
+            nc.sync.dma_start(
+                out=x_sb[b][:, j, :],
+                in_=x[b].rearrange("(p j) k -> p j k", j=TOK)[:, j, :],
+            )
 
-        for quad in range(QUADS):
-            nc.sync.dma_start(
-                out=wa_planes[32 * quad : 32 * quad + 16, :].bitcast(I32),
-                in_=Wkva_scales[:, 4 * quad : 4 * quad + 4, :].bitcast(I32),
-            )
-        load_x(0)
-        for g in range(GROUPS):
-            nc.sync.dma_start(
-                out=wa_words[:, g, :].bitcast(I32),
-                in_=Wkva_words[g].rearrange("p n t -> p (n t)").bitcast(I32),
-            )
-        for quad in range(QUADS):
-            nc.sync.dma_start(
-                out=wb_planes[32 * quad : 32 * quad + 16, :].bitcast(I32),
-                in_=Wkvb_scales[0, 4 * quad : 4 * quad + 4, :]
-                .rearrange("r (c n) -> c r n", c=PLANES)
-                .bitcast(I32),
-            )
-        nc.sync.dma_start(out=gain_bf[:], in_=kv_a_norm_w.rearrange("(p t) -> p t", t=PACK))
-        wb_dram = Wkvb_words[0].rearrange("p n t -> p (n t)").bitcast(I32)
-        for c in range(PLANES):
-            cols = slice(c * B_PLANE_COLS, (c + 1) * B_PLANE_COLS)
-            nc.sync.dma_start(out=wb_words[:, cols].bitcast(I32), in_=wb_dram[:, cols])
-        load_x(1)
+        with tc.manual_schedule(engines={mybir.EngineType.SP}):
+            load_x(0, 0)
+            for quad in range(QUADS):
+                nc.sync.dma_start(
+                    out=wa_planes[32 * quad : 32 * quad + 16, :].bitcast(I32),
+                    in_=Wkva_scales[:, 4 * quad : 4 * quad + 4, :].bitcast(I32),
+                )
+            load_x(0, 1)
+            for g in range(GROUPS):
+                nc.sync.dma_start(
+                    out=wa_words[:, g, :].bitcast(I32),
+                    in_=Wkva_words[g].rearrange("p n t -> p (n t)").bitcast(I32),
+                )
+            for quad in range(QUADS):
+                nc.sync.dma_start(
+                    out=wb_planes[32 * quad : 32 * quad + 16, :].bitcast(I32),
+                    in_=Wkvb_scales[0, 4 * quad : 4 * quad + 4, :]
+                    .rearrange("r (c n) -> c r n", c=PLANES)
+                    .bitcast(I32),
+                )
+            nc.sync.dma_start(out=gain_bf[:], in_=kv_a_norm_w.rearrange("(p t) -> p t", t=PACK))
+            wb_dram = Wkvb_words[0].rearrange("p n t -> p (n t)").bitcast(I32)
+            for c in range(PLANES):
+                cols = slice(c * B_PLANE_COLS, (c + 1) * B_PLANE_COLS)
+                nc.sync.dma_start(out=wb_words[:, cols].bitcast(I32), in_=wb_dram[:, cols])
+            load_x(1, 0)
+            load_x(1, 1)
 
         ident = const.tile([P, P], F32)
         make_identity(nc, ident[:])
@@ -159,12 +158,14 @@ def tile_multiheadlatentattention_pb_kernel(
         warm = const.tile([P, 1], F32)
         nc.scalar.activation(out=warm[:], in_=tab[:, 0, 0:1], func=ACT.Sqrt, bias=1.0, scale=0.0)
 
-        def quantise_x(b, j):
+        def quantise_x(b, j, bank_pool, bank_tag):
             x_words = x_sb[b][:].bitcast(F32)
             grouped = xq.tile([P, GROUPS, P, PACK], BF16, align_bytes=64)
             grouped_words = grouped[:].bitcast(F32)
+            codes = xq.tile([P, GROUPS * P], U32, align_bytes=64)
+            scales = xq.tile([P, GROUPS * P], U8, align_bytes=64)
             for half in range(GROUPS // 2):
-                xt = tp_ps.tile([P, 2, 2, P], F32, tag="tp")
+                xt = bank_pool.tile([P, 2, 2, P], F32, tag=bank_tag, name="xt")
                 for gi in range(2):
                     g = 2 * half + gi
                     for u in range(2):
@@ -178,13 +179,12 @@ def tile_multiheadlatentattention_pb_kernel(
                     out=grouped_words[:, 2 * half : 2 * half + 2, :, :],
                     in_=xt[:].rearrange("p g u k -> p g k u"),
                 )
-            codes = xq.tile([P, GROUPS * P], U32, align_bytes=64)
-            scales = xq.tile([P, GROUPS * P], U8, align_bytes=64)
-            nc.vector.quantize_mx(
-                out=codes[:].bitcast(FP8X4),
-                scales=scales[:],
-                in_=grouped[:].rearrange("p g k t -> p (g k t)"),
-            )
+                cols = slice(2 * half * P, 2 * (half + 1) * P)
+                nc.vector.quantize_mx(
+                    out=codes[:, cols].bitcast(FP8X4),
+                    scales=scales[:, cols],
+                    in_=grouped[:, 2 * half : 2 * half + 2, :, :].rearrange("p g k t -> p (g k t)"),
+                )
             return codes, scales
 
         def first_pass(x_mx_j, g, n_cols, acc):
@@ -199,38 +199,67 @@ def tile_multiheadlatentattention_pb_kernel(
                 stop=(g == GROUPS - 1),
             )
 
+        def first_matmul(x_mx):
+            latent = []
+            for j in range(TOK):
+                latent_j = lat_ps.tile([P, LATENT], F32, name="latent_j")
+                latent.append(latent_j)
+            for g in range(GROUPS):
+                for j in range(TOK):
+                    first_pass(x_mx[j], g, slice(0, LATENT), latent[j][:])
+            r_bank = rope_ps.tile([P, 512], F32)
+            for j in range(TOK):
+                for g in range(GROUPS):
+                    first_pass(x_mx[j], g, slice(LATENT, A_COLS), r_bank[:, j * ROPE : (j + 1) * ROPE])
+            return latent, r_bank
+
         def quantise_h(latent):
-            squares = norm.tile([P, LATENT], BF16)
-            mean_sq = norm.tile([P, 1], F32)
-            nc.scalar.activation(
-                out=squares[:], in_=latent[:], func=ACT.Square,
-                scale=1.0 / math.sqrt(LATENT), accum_out=mean_sq[:],
-            )
-            rms = norm.tile([P, 1], F32)
-            nc.scalar.activation(out=rms[:], in_=mean_sq[:], func=ACT.Sqrt, bias=EPS, scale=1.0)
-            rstd = norm.tile([P, 1], F32)
-            nc.vector.reciprocal(out=rstd[:], in_=rms[:])
-            normed = norm.tile([P, PACK, P], F32)
-            nc.vector.tensor_scalar(
-                out=normed[:], in0=latent[:].rearrange("p (q t) -> p t q", t=PACK),
-                scalar1=rstd[:, 0:1], scalar2=None, op0=ALU.mult,
-            )
-            normed_t = tp_ps.tile([P, PACK, P], F32, tag="tp")
-            for t in range(PACK):
-                nc.tensor.transpose(out=normed_t[:, t, :], in_=normed[:, t, :], identity=ident[:])
-            h_grouped = norm.tile([P, P, PACK], BF16, align_bytes=64)
-            nc.vector.tensor_tensor(
-                out=h_grouped[:], in0=normed_t[:].rearrange("p t k -> p k t"),
-                in1=gain[:].unsqueeze(1).to_broadcast([P, P, PACK]), op=ALU.mult,
-            )
-            codes = norm.tile([P, P], U32, align_bytes=64)
-            scales = norm.tile([P, P], U8, align_bytes=64)
-            nc.vector.quantize_mx(
-                out=codes[:].bitcast(FP8X4),
-                scales=scales[:],
-                in_=h_grouped[:].rearrange("p k t -> p (k t)"),
-            )
-            return codes, scales
+            rms = []
+            for j in range(TOK):
+                squares = norm.tile([P, LATENT], BF16)
+                mean_sq = norm.tile([P, 1], F32)
+                nc.scalar.activation(
+                    out=squares[:], in_=latent[j][:], func=ACT.Square,
+                    scale=1.0 / math.sqrt(LATENT), accum_out=mean_sq[:],
+                )
+                rms_j = norm.tile([P, 1], F32, name="rms_j")
+                nc.scalar.activation(out=rms_j[:], in_=mean_sq[:], func=ACT.Sqrt, bias=EPS, scale=1.0)
+                rms.append(rms_j)
+            normed = []
+            for j in range(TOK):
+                rstd = norm.tile([P, 1], F32)
+                nc.vector.reciprocal(out=rstd[:], in_=rms[j][:])
+                normed_j = norm.tile([P, PACK, P], F32, name="normed_j")
+                nc.vector.tensor_scalar(
+                    out=normed_j[:], in0=latent[j][:].rearrange("p (q t) -> p t q", t=PACK),
+                    scalar1=rstd[:, 0:1], scalar2=None, op0=ALU.mult,
+                )
+                normed.append(normed_j)
+            normed_t = []
+            for j in range(TOK):
+                normed_t_j = tp_ps.tile([P, PACK, P], F32, tag="tp", name="normed_t_j")
+                for t in range(PACK):
+                    nc.tensor.transpose(out=normed_t_j[:, t, :], in_=normed[j][:, t, :], identity=ident[:])
+                normed_t.append(normed_t_j)
+            h_grouped = []
+            for j in range(TOK):
+                h_grouped_j = norm.tile([P, P, PACK], BF16, align_bytes=64, name="h_grouped_j")
+                nc.vector.tensor_tensor(
+                    out=h_grouped_j[:], in0=normed_t[j][:].rearrange("p t k -> p k t"),
+                    in1=gain[:].unsqueeze(1).to_broadcast([P, P, PACK]), op=ALU.mult,
+                )
+                h_grouped.append(h_grouped_j)
+            h_mx = []
+            for j in range(TOK):
+                codes = norm.tile([P, P], U32, align_bytes=64)
+                scales = norm.tile([P, P], U8, align_bytes=64)
+                nc.vector.quantize_mx(
+                    out=codes[:].bitcast(FP8X4),
+                    scales=scales[:],
+                    in_=h_grouped[j][:].rearrange("p k t -> p (k t)"),
+                )
+                h_mx.append((codes, scales))
+            return h_mx
 
         def rotate(r_bank):
             prod = rope.tile([P, 2, TOK * ROPE], F32)
@@ -248,13 +277,6 @@ def tile_multiheadlatentattention_pb_kernel(
                 )
             return rotated
 
-        def store_rope(b, rotated):
-            for j in range(TOK):
-                nc.sync.dma_start(
-                    out=out_0[b].rearrange("h (p j) d -> p h j d", j=TOK)[:, :, j, NOPE:K_OUT],
-                    in_=rotated[:, j, :].unsqueeze(1).to_broadcast([P, HEADS, ROPE]),
-                )
-
         def spread_rope(rotated, k_rows):
             for pair in range(N_PAIRS):
                 heads = slice(PAIR * pair, PAIR * (pair + 1))
@@ -264,65 +286,63 @@ def tile_multiheadlatentattention_pb_kernel(
                     scalar1=1.0, scalar2=0.0, op0=ALU.mult, op1=ALU.add,
                 )
 
-        def second_matmul(b, h_mx, k_sb, v_sb):
-            for pair in range(N_PAIRS):
-                heads = slice(PAIR * pair, PAIR * (pair + 1))
-                plane = (pair * PAIR_COLS) // B_PLANE_COLS
-                in_plane = (pair * PAIR_COLS) % B_PLANE_COLS
-                for j in range(TOK):
-                    codes, scales = h_mx[j]
-                    kv = kv_ps.tile([P, 512], F32)
-                    for lo, hi in ((0, 256), (256, PAIR_COLS)):
-                        nc.tensor.matmul_mx(
-                            out=kv[:, lo:hi],
-                            lhsT=codes[:].bitcast(FP8X4),
-                            lhsT_scale=scales[:],
-                            rhs=wb_words[:, pair * PAIR_COLS + lo : pair * PAIR_COLS + hi].bitcast(FP8X4),
-                            rhs_scale=wb_planes[4 * plane : P, in_plane + lo : in_plane + hi],
-                            start=True,
-                            stop=True,
-                        )
-                    by_head = kv[:, 0:PAIR_COLS].rearrange("p (h c) -> p h c", h=PAIR)
-                    copy = nc.vector.tensor_copy if j == 0 else nc.scalar.copy
-                    copy(out=k_sb[:, heads, j, 0:NOPE], in_=by_head[:, :, 0:NOPE])
-                    copy(out=v_sb[:, heads, j, :], in_=by_head[:, :, NOPE:HEAD_COLS])
-                if b >= EARLY_ROPE:
-                    nc.sync.dma_start(
-                        out=out_0[b, heads].rearrange("h (p j) d -> p h (j d)", j=TOK),
-                        in_=k_sb[:, heads, :, :].rearrange("p h j d -> p h (j d)"),
+        def second_matmul(b, pair, h_mx, k_sb, v_sb):
+            heads = slice(PAIR * pair, PAIR * (pair + 1))
+            plane = (pair * PAIR_COLS) // B_PLANE_COLS
+            in_plane = (pair * PAIR_COLS) % B_PLANE_COLS
+            for j in range(TOK):
+                codes, scales = h_mx[j]
+                kv = kv_ps.tile([P, 512], F32, tag="kv")
+                for lo, hi in ((0, 256), (256, PAIR_COLS)):
+                    nc.tensor.matmul_mx(
+                        out=kv[:, lo:hi],
+                        lhsT=codes[:].bitcast(FP8X4),
+                        lhsT_scale=scales[:],
+                        rhs=wb_words[:, pair * PAIR_COLS + lo : pair * PAIR_COLS + hi].bitcast(FP8X4),
+                        rhs_scale=wb_planes[4 * plane : P, in_plane + lo : in_plane + hi],
+                        start=True,
+                        stop=True,
                     )
-                elif pair % NOPE_STORE_PAIRS == NOPE_STORE_PAIRS - 1:
-                    done = slice(PAIR * (pair + 1 - NOPE_STORE_PAIRS), PAIR * (pair + 1))
-                    for j in range(TOK):
-                        nc.sync.dma_start(
-                            out=out_0[b, done].rearrange("h (p j) d -> p h j d", j=TOK)[:, :, j, 0:NOPE],
-                            in_=k_sb[:, done, j, :],
-                        )
-                nc.sync.dma_start(
-                    out=out_1[b, heads].rearrange("h (p j) d -> p h (j d)", j=TOK),
-                    in_=v_sb[:, heads, :, :].rearrange("p h j d -> p h (j d)"),
-                )
+                by_head = kv[:, 0:PAIR_COLS].rearrange("p (h c) -> p h c", h=PAIR)
+                copy = nc.vector.tensor_copy if j == 0 else nc.scalar.copy
+                copy(out=v_sb[:, heads, j, :], in_=by_head[:, :, NOPE:HEAD_COLS])
+                copy(out=k_sb[:, heads, j, 0:NOPE], in_=by_head[:, :, 0:NOPE])
+            nc.sync.dma_start(
+                out=out_1[b, heads].rearrange("h (p j) d -> p h (j d)", j=TOK),
+                in_=v_sb[:, heads, :, :].rearrange("p h j d -> p h (j d)"),
+            )
+            nc.sync.dma_start(
+                out=out_0[b, heads].rearrange("h (p j) d -> p h (j d)", j=TOK),
+                in_=k_sb[:, heads, :, :].rearrange("p h j d -> p h (j d)"),
+            )
 
+        k_sb = []
+        v_sb = []
         for b in range(BATCH):
-            x_mx = [quantise_x(b, j) for j in range(TOK)]
-            latent = []
-            for j in range(TOK):
-                latent_j = lat_ps.tile([P, LATENT], F32, name="latent_j")
-                latent.append(latent_j)
-            for g in range(GROUPS):
-                for j in range(TOK):
-                    first_pass(x_mx[j], g, slice(0, LATENT), latent[j][:])
-            r_bank = rope_ps.tile([P, 512], F32)
-            for j in range(TOK):
-                for g in range(GROUPS):
-                    first_pass(x_mx[j], g, slice(LATENT, A_COLS), r_bank[:, j * ROPE : (j + 1) * ROPE])
-            h_mx = [quantise_h(latent[j]) for j in range(TOK)]
-            rotated = rotate(r_bank[:, 0 : TOK * ROPE])
-            if b < EARLY_ROPE:
-                store_rope(b, rotated)
-                k_sb = outs.tile([P, HEADS, TOK, NOPE], F32, name="k_nope_sb", bufs=1)
-            else:
-                k_sb = outs.tile([P, HEADS, TOK, K_OUT], F32, name="k_sb", bufs=1)
-                spread_rope(rotated, k_sb)
-            v_sb = outs.tile([P, HEADS, TOK, VDIM], F32)
-            second_matmul(b, h_mx, k_sb, v_sb)
+            k_b = outs.tile([P, HEADS, TOK, K_OUT], F32, name="k_b")
+            v_b = outs.tile([P, HEADS, TOK, VDIM], F32, name="v_b")
+            k_sb.append(k_b)
+            v_sb.append(v_b)
+
+        x_mx = [quantise_x(0, 0, tp_ps, "tp"), quantise_x(0, 1, kv_ps, "kv")]
+        latent, r_bank = first_matmul(x_mx)
+        h_mx = quantise_h(latent)
+        rotated = rotate(r_bank[:, 0 : TOK * ROPE])
+        spread_rope(rotated, k_sb[0])
+
+        second_matmul(0, 0, h_mx, k_sb[0], v_sb[0])
+        second_matmul(0, 1, h_mx, k_sb[0], v_sb[0])
+        x_mx_1 = [quantise_x(1, 0, tp_ps, "tp")]
+        second_matmul(0, 2, h_mx, k_sb[0], v_sb[0])
+        x_mx_1.append(quantise_x(1, 1, tp_ps, "tp"))
+        second_matmul(0, 3, h_mx, k_sb[0], v_sb[0])
+        latent_1, r_bank_1 = first_matmul(x_mx_1)
+        second_matmul(0, 4, h_mx, k_sb[0], v_sb[0])
+        h_mx_1 = quantise_h(latent_1)
+        second_matmul(0, 5, h_mx, k_sb[0], v_sb[0])
+        rotated_1 = rotate(r_bank_1[:, 0 : TOK * ROPE])
+        spread_rope(rotated_1, k_sb[1])
+        second_matmul(0, 6, h_mx, k_sb[0], v_sb[0])
+        second_matmul(0, 7, h_mx, k_sb[0], v_sb[0])
+        for pair in range(N_PAIRS):
+            second_matmul(1, pair, h_mx_1, k_sb[1], v_sb[1])

@@ -36,6 +36,10 @@ QUADS = 4
 PLANES = 4
 B_PLANE_COLS = B_COLS // PLANES
 
+WARM_START = 6
+WARM_BETWEEN = 2
+WARM_NORM = 1
+
 ROUND_MAGIC = 1.5 * 2.0**23
 
 FLOPS = 2 * BATCH * SEQ * (D_MODEL * A_COLS + LATENT * B_COLS)
@@ -56,6 +60,13 @@ def tile_multiheadlatentattention_pb_kernel(
         lat_ps = ctx.enter_context(tc.psum_pool(name="lat_ps", bufs=TOK))
         rope_ps = ctx.enter_context(tc.psum_pool(name="rope_ps", bufs=1))
         kv_ps = ctx.enter_context(tc.psum_pool(name="kv_ps", bufs=3))
+
+        zeros = const.tile([P, 512], BF16)
+        nc.vector.memset(zeros[:], 0.0)
+
+        def keep_warm(moving, count, bank):
+            for i in range(count):
+                nc.tensor.matmul(out=bank, lhsT=zeros[:, 0:P], rhs=moving, start=True, stop=True)
 
         wa_planes = const.tile([P, A_COLS], U8, align_bytes=64)
         wb_planes = const.tile([P, B_PLANE_COLS], U8, align_bytes=64)
@@ -151,14 +162,9 @@ def tile_multiheadlatentattention_pb_kernel(
             op0=ALU.subtract, op1=ALU.subtract,
         )
         tab = const.tile([P, 2, TOK * ROPE], F32)
-        nc.scalar.activation(
-            out=tab[:].rearrange("p c f -> p (c f)"), in_=minus_frac[:], func=ACT.Sin,
-            scale=-2.0 * math.pi,
-        )
-        warm = const.tile([P, 1], F32)
-        nc.scalar.activation(out=warm[:], in_=tab[:, 0, 0:1], func=ACT.Sqrt, bias=1.0, scale=0.0)
+        warm = const.tile([P, 2], F32)
 
-        def quantise_x(b, j, bank_pool, bank_tag):
+        def quantise_x(b, j, bank_pool, bank_tag, warm_bank=None):
             x_words = x_sb[b][:].bitcast(F32)
             grouped = xq.tile([P, GROUPS, P, PACK], BF16, align_bytes=64)
             grouped_words = grouped[:].bitcast(F32)
@@ -185,6 +191,8 @@ def tile_multiheadlatentattention_pb_kernel(
                     scales=scales[:, cols],
                     in_=grouped[:, 2 * half : 2 * half + 2, :, :].rearrange("p g k t -> p (g k t)"),
                 )
+            if warm_bank is not None:
+                keep_warm(grouped[:, 0, :, :].rearrange("p k t -> p (k t)"), WARM_BETWEEN, warm_bank)
             return codes, scales
 
         def first_pass(x_mx_j, g, n_cols, acc):
@@ -207,13 +215,13 @@ def tile_multiheadlatentattention_pb_kernel(
             for g in range(GROUPS):
                 for j in range(TOK):
                     first_pass(x_mx[j], g, slice(0, LATENT), latent[j][:])
-            r_bank = rope_ps.tile([P, 512], F32)
+            r_bank = rope_ps.tile([P, 512], F32, tag="rope")
             for j in range(TOK):
                 for g in range(GROUPS):
                     first_pass(x_mx[j], g, slice(LATENT, A_COLS), r_bank[:, j * ROPE : (j + 1) * ROPE])
             return latent, r_bank
 
-        def quantise_h(latent):
+        def quantise_h(latent, warm_bank=None):
             rms = []
             for j in range(TOK):
                 squares = norm.tile([P, LATENT], BF16)
@@ -225,6 +233,8 @@ def tile_multiheadlatentattention_pb_kernel(
                 rms_j = norm.tile([P, 1], F32, name="rms_j")
                 nc.scalar.activation(out=rms_j[:], in_=mean_sq[:], func=ACT.Sqrt, bias=EPS, scale=1.0)
                 rms.append(rms_j)
+                if warm_bank is not None:
+                    keep_warm(squares[:], WARM_NORM, warm_bank)
             normed = []
             for j in range(TOK):
                 rstd = norm.tile([P, 1], F32)
@@ -249,6 +259,8 @@ def tile_multiheadlatentattention_pb_kernel(
                     in1=gain[:].unsqueeze(1).to_broadcast([P, P, PACK]), op=ALU.mult,
                 )
                 h_grouped.append(h_grouped_j)
+                if warm_bank is not None and j == 0:
+                    keep_warm(h_grouped_j[:].rearrange("p k t -> p (k t)"), WARM_NORM, warm_bank)
             h_mx = []
             for j in range(TOK):
                 codes = norm.tile([P, P], U32, align_bytes=64)
@@ -272,7 +284,7 @@ def tile_multiheadlatentattention_pb_kernel(
             rotated = rope.tile([P, TOK, ROPE], F32)
             rotated_pairs = rotated[:].rearrange("p j (m e) -> p (j m) e", e=2)
             for e in range(2):
-                nc.vector.tensor_tensor(
+                nc.gpsimd.tensor_tensor(
                     out=rotated_pairs[:, :, e], in0=own[:, :, e], in1=carry[:, :, 1 - e], op=ALU.add
                 )
             return rotated
@@ -311,6 +323,9 @@ def tile_multiheadlatentattention_pb_kernel(
                 out=out_1[b, heads].rearrange("h (p j) d -> p h (j d)", j=TOK),
                 in_=v_sb[:, heads, :, :].rearrange("p h j d -> p h (j d)"),
             )
+
+        def store_k(b, pair, k_sb):
+            heads = slice(PAIR * pair, PAIR * (pair + 1))
             nc.sync.dma_start(
                 out=out_0[b, heads].rearrange("h (p j) d -> p h (j d)", j=TOK),
                 in_=k_sb[:, heads, :, :].rearrange("p h j d -> p h (j d)"),
@@ -324,25 +339,44 @@ def tile_multiheadlatentattention_pb_kernel(
             k_sb.append(k_b)
             v_sb.append(v_b)
 
-        x_mx = [quantise_x(0, 0, tp_ps, "tp"), quantise_x(0, 1, kv_ps, "kv")]
-        latent, r_bank = first_matmul(x_mx)
-        h_mx = quantise_h(latent)
-        rotated = rotate(r_bank[:, 0 : TOK * ROPE])
-        spread_rope(rotated, k_sb[0])
+        with tc.manual_schedule(engines={mybir.EngineType.Activation}):
+            nc.scalar.activation(out=warm[:, 0:1], in_=turns[:, 0:1], func=ACT.Sqrt, bias=1.0, scale=0.0)
+            warm_first = rope_ps.tile([P, 512], F32, tag="rope")
+            keep_warm(zeros[:], WARM_START, warm_first[:])
+            x_mx = [quantise_x(0, 0, tp_ps, "tp", warm_first[:]), quantise_x(0, 1, kv_ps, "kv")]
+            latent, r_bank = first_matmul(x_mx)
+            warm_later = kv_ps.tile([P, 512], F32, tag="kv")
+            h_mx = quantise_h(latent, warm_later[:])
+            nc.scalar.activation(
+                out=tab[:].rearrange("p c f -> p (c f)"), in_=minus_frac[:], func=ACT.Sin,
+                scale=-2.0 * math.pi,
+            )
+            nc.scalar.activation(out=warm[:, 1:2], in_=tab[:, 0, 0:1], func=ACT.Sqrt, bias=1.0, scale=0.0)
 
         second_matmul(0, 0, h_mx, k_sb[0], v_sb[0])
         second_matmul(0, 1, h_mx, k_sb[0], v_sb[0])
+        rotated = rotate(r_bank[:, 0 : TOK * ROPE])
+        spread_rope(rotated, k_sb[0])
         x_mx_1 = [quantise_x(1, 0, tp_ps, "tp")]
         second_matmul(0, 2, h_mx, k_sb[0], v_sb[0])
         x_mx_1.append(quantise_x(1, 1, tp_ps, "tp"))
         second_matmul(0, 3, h_mx, k_sb[0], v_sb[0])
+        store_k(0, 0, k_sb[0])
         latent_1, r_bank_1 = first_matmul(x_mx_1)
         second_matmul(0, 4, h_mx, k_sb[0], v_sb[0])
+        store_k(0, 1, k_sb[0])
         h_mx_1 = quantise_h(latent_1)
         second_matmul(0, 5, h_mx, k_sb[0], v_sb[0])
+        store_k(0, 2, k_sb[0])
         rotated_1 = rotate(r_bank_1[:, 0 : TOK * ROPE])
         spread_rope(rotated_1, k_sb[1])
         second_matmul(0, 6, h_mx, k_sb[0], v_sb[0])
+        store_k(0, 3, k_sb[0])
         second_matmul(0, 7, h_mx, k_sb[0], v_sb[0])
+        store_k(0, 4, k_sb[0])
+        store_k(0, 5, k_sb[0])
+        store_k(0, 6, k_sb[0])
+        store_k(0, 7, k_sb[0])
         for pair in range(N_PAIRS):
             second_matmul(1, pair, h_mx_1, k_sb[1], v_sb[1])
+            store_k(1, pair, k_sb[1])

@@ -36,7 +36,7 @@ QUADS = 4
 PLANES = 4
 B_PLANE_COLS = B_COLS // PLANES
 
-WARM_START = 6
+WARM_START = 5
 WARM_BETWEEN = 2
 WARM_NORM = 1
 
@@ -81,25 +81,33 @@ def tile_multiheadlatentattention_pb_kernel(
             x_b = xin.tile([P, TOK, D_MODEL], BF16, name="x_b")
             x_sb.append(x_b)
 
-        def load_x(b, j):
-            nc.sync.dma_start(
-                out=x_sb[b][:, j, :],
-                in_=x[b].rearrange("(p j) k -> p j k", j=TOK)[:, j, :],
-            )
+        def load_x(b, j, pieces=1):
+            width = D_MODEL // pieces
+            for piece in range(pieces):
+                cols = slice(piece * width, (piece + 1) * width)
+                nc.sync.dma_start(
+                    out=x_sb[b][:, j, cols],
+                    in_=x[b].rearrange("(p j) k -> p j k", j=TOK)[:, j, cols],
+                )
 
         with tc.manual_schedule(engines={mybir.EngineType.SP}):
-            load_x(0, 0)
+            load_x(0, 0, pieces=2)
             for quad in range(QUADS):
                 nc.sync.dma_start(
                     out=wa_planes[32 * quad : 32 * quad + 16, :].bitcast(I32),
                     in_=Wkva_scales[:, 4 * quad : 4 * quad + 4, :].bitcast(I32),
                 )
-            load_x(0, 1)
+            load_x(0, 1, pieces=2)
+            wa_dram = Wkva_words.rearrange("g p n t -> p g (n t)")
             for g in range(GROUPS):
                 nc.sync.dma_start(
-                    out=wa_words[:, g, :].bitcast(I32),
-                    in_=Wkva_words[g].rearrange("p n t -> p (n t)").bitcast(I32),
+                    out=wa_words[:, g, 0:LATENT].bitcast(I32),
+                    in_=wa_dram[:, g, 0 : PACK * LATENT].bitcast(I32),
                 )
+            nc.sync.dma_start(
+                out=wa_words[:, :, LATENT:A_COLS].bitcast(I32),
+                in_=wa_dram[:, :, PACK * LATENT : PACK * A_COLS].bitcast(I32),
+            )
             for quad in range(QUADS):
                 nc.sync.dma_start(
                     out=wb_planes[32 * quad : 32 * quad + 16, :].bitcast(I32),

@@ -19,6 +19,7 @@ K_PASS = P * PACK
 
 BATCH, SEQ, D_MODEL = 2, 256, 2048
 LATENT, ROPE = 512, 128
+HALF = ROPE // 2
 HEADS, NOPE, VDIM = 16, 64, 128
 A_COLS = LATENT + ROPE
 HEAD_COLS = NOPE + VDIM
@@ -36,8 +37,8 @@ QUADS = 4
 PLANES = 4
 B_PLANE_COLS = B_COLS // PLANES
 
+
 WARM_START = 5
-WARM_BETWEEN = 2
 WARM_NORM = 1
 
 ROUND_MAGIC = 1.5 * 2.0**23
@@ -61,36 +62,42 @@ def tile_multiheadlatentattention_pb_kernel(
         rope_ps = ctx.enter_context(tc.psum_pool(name="rope_ps", bufs=1))
         kv_ps = ctx.enter_context(tc.psum_pool(name="kv_ps", bufs=3))
 
-        zeros = const.tile([P, 512], BF16)
-        nc.vector.memset(zeros[:], 0.0)
+        with tc.manual_schedule():
 
-        def keep_warm(moving, count, bank):
-            for i in range(count):
-                nc.tensor.matmul(out=bank, lhsT=zeros[:, 0:P], rhs=moving, start=True, stop=True)
+            zeros = const.tile([P, 512], BF16)
+            nc.gpsimd.memset(zeros[:].bitcast(F32), 0.0)
+            position = const.tile([P, TOK], I32)
+            nc.gpsimd.iota(position[:], pattern=[[1, TOK]], base=0, channel_multiplier=TOK)
 
-        wa_planes = const.tile([P, A_COLS], U8, align_bytes=64)
-        wb_planes = const.tile([P, B_PLANE_COLS], U8, align_bytes=64)
-        nc.gpsimd.memset(wa_planes[:].bitcast(F32), 0.0)
-        nc.gpsimd.memset(wb_planes[:].bitcast(F32), 0.0)
+            def keep_warm(moving, count, bank):
+                for i in range(count):
+                    nc.tensor.matmul(out=bank, lhsT=zeros[:, 0:P], rhs=moving, start=True, stop=True)
 
-        wa_words = const.tile([P, GROUPS, A_COLS], U32, align_bytes=64)
-        wb_words = const.tile([P, B_COLS], U32, align_bytes=64)
-        gain_bf = const.tile([P, PACK], BF16)
-        x_sb = []
-        for b in range(BATCH):
-            x_b = xin.tile([P, TOK, D_MODEL], BF16, name="x_b")
-            x_sb.append(x_b)
+            wa_planes = const.tile([P, A_COLS], U8, align_bytes=64)
+            wb_planes = const.tile([P, B_PLANE_COLS], U8, align_bytes=64)
+            nc.gpsimd.memset(wa_planes[:].bitcast(F32), 0.0)
+            ident = const.tile([P, P], F32)
+            make_identity(nc, ident[:])
+            gain_row = const.tile([P, LATENT], BF16)
+            nc.gpsimd.memset(gain_row[:].bitcast(F32), 0.0)
+            nc.gpsimd.memset(wb_planes[:].bitcast(F32), 0.0)
 
-        def load_x(b, j, pieces=1):
-            width = D_MODEL // pieces
-            for piece in range(pieces):
-                cols = slice(piece * width, (piece + 1) * width)
-                nc.sync.dma_start(
-                    out=x_sb[b][:, j, cols],
-                    in_=x[b].rearrange("(p j) k -> p j k", j=TOK)[:, j, cols],
-                )
+            wa_words = const.tile([P, GROUPS, A_COLS], U32, align_bytes=64)
+            wb_words = const.tile([P, B_COLS], U32, align_bytes=64)
+            x_sb = []
+            for b in range(BATCH):
+                x_b = xin.tile([P, TOK, D_MODEL], BF16, name="x_b")
+                x_sb.append(x_b)
 
-        with tc.manual_schedule(engines={mybir.EngineType.SP}):
+            def load_x(b, j, pieces=1):
+                width = D_MODEL // pieces
+                for piece in range(pieces):
+                    cols = slice(piece * width, (piece + 1) * width)
+                    nc.sync.dma_start(
+                        out=x_sb[b][:, j, cols],
+                        in_=x[b].rearrange("(p j) k -> p j k", j=TOK)[:, j, cols],
+                    )
+
             load_x(0, 0, pieces=2)
             for quad in range(QUADS):
                 nc.sync.dma_start(
@@ -104,6 +111,8 @@ def tile_multiheadlatentattention_pb_kernel(
                     out=wa_words[:, g, 0:LATENT].bitcast(I32),
                     in_=wa_dram[:, g, 0 : PACK * LATENT].bitcast(I32),
                 )
+                if g == 0:
+                    nc.sync.dma_start(out=gain_row[0:1, :], in_=kv_a_norm_w.rearrange("(o n) -> o n", o=1))
             nc.sync.dma_start(
                 out=wa_words[:, :, LATENT:A_COLS].bitcast(I32),
                 in_=wa_dram[:, :, PACK * LATENT : PACK * A_COLS].bitcast(I32),
@@ -115,71 +124,78 @@ def tile_multiheadlatentattention_pb_kernel(
                     .rearrange("r (c n) -> c r n", c=PLANES)
                     .bitcast(I32),
                 )
-            nc.sync.dma_start(out=gain_bf[:], in_=kv_a_norm_w.rearrange("(p t) -> p t", t=PACK))
             wb_dram = Wkvb_words[0].rearrange("p n t -> p (n t)").bitcast(I32)
             for c in range(PLANES):
                 cols = slice(c * B_PLANE_COLS, (c + 1) * B_PLANE_COLS)
                 nc.sync.dma_start(out=wb_words[:, cols].bitcast(I32), in_=wb_dram[:, cols])
-            load_x(1, 0)
-            load_x(1, 1)
+                if c < TOK:
+                    load_x(1, c)
 
-        ident = const.tile([P, P], F32)
-        make_identity(nc, ident[:])
-        gain = const.tile([P, PACK], F32)
-        nc.vector.tensor_copy(out=gain[:], in_=gain_bf[:])
+            powers = const.tile([P, 2, 8], F32)
+            nc.vector.memset(powers[:, :, 0:1], 1.0)
+            ones = const.tile([P, P], BF16)
+            nc.vector.memset(ones[:], 1.0)
+            for step in range(3):
+                n = 2**step
+                for row in range(2):
+                    nc.vector.tensor_scalar(
+                        out=powers[:, row, n : 2 * n], in0=powers[:, row, 0:n],
+                        scalar1=math.pow(THETA, -n * 8**row / 64.0), scalar2=None, op0=ALU.mult,
+                    )
+                if step == 0:
+                    turns = const.tile([P, 2, TOK], F32)
+                    for row in range(2):
+                        nc.vector.tensor_scalar(
+                            out=turns[:, row, :], in0=position[:],
+                            scalar1=(1 - 2 * row) / (2.0 * math.pi), scalar2=None, op0=ALU.mult,
+                        )
+            freq = const.tile([P, HALF], F32)
+            nc.vector.tensor_tensor(
+                out=freq[:].rearrange("p (a i) -> p a i", i=8),
+                in0=powers[:, 1, :].unsqueeze(2).to_broadcast([P, 8, 8]),
+                in1=powers[:, 0, :].unsqueeze(1).to_broadcast([P, 8, 8]), op=ALU.mult,
+            )
+            freq_pairs = freq[:].rearrange("p (m e) -> p m e", e=2)
+            angle = const.tile([P, 2, TOK, HALF], F32)
+            for j in range(TOK):
+                nc.vector.tensor_scalar(
+                    out=angle[:, 0, j, :], in0=freq[:],
+                    scalar1=turns[:, 0, j : j + 1], scalar2=0.25, op0=ALU.mult, op1=ALU.add,
+                )
+                carried = angle[:, 1, j, :].rearrange("p (m e) -> p m e", e=2)
+                for e in range(2):
+                    nc.vector.tensor_scalar(
+                        out=carried[:, :, e], in0=freq_pairs[:, :, 1 - e],
+                        scalar1=turns[:, e, j : j + 1], scalar2=None, op0=ALU.mult,
+                    )
+            angle_flat = angle[:].rearrange("p c j f -> p (c j f)")
+            shifted = const.tile([P, 2 * TOK * HALF], F32)
+            nc.vector.tensor_scalar(
+                out=shifted[:], in0=angle_flat, scalar1=ROUND_MAGIC, scalar2=None, op0=ALU.add
+            )
+            minus_frac = const.tile([P, 2 * TOK * HALF], F32)
+            nc.vector.scalar_tensor_tensor(
+                out=minus_frac[:], in0=shifted[:], scalar=ROUND_MAGIC, in1=angle_flat,
+                op0=ALU.subtract, op1=ALU.subtract,
+            )
+            tab = const.tile([P, 2, TOK, HALF], F32)
+            warm = const.tile([P, 2], F32)
+            nc.scalar.activation(out=warm[:, 0:1], in_=powers[:, 0, 0:1], func=ACT.Sin, scale=0.0)
+            nc.scalar.activation(
+                out=tab[:].rearrange("p c j f -> p (c j f)"), in_=minus_frac[:], func=ACT.Sin,
+                scale=-2.0 * math.pi,
+            )
 
-        freq = const.tile([P, ROPE], F32)
-        nc.vector.memset(freq[:, 0:1], 1.0)
-        for step in range(6):
-            n = 2**step
-            nc.vector.tensor_scalar(
-                out=freq[:, n : 2 * n], in0=freq[:, 0:n],
-                scalar1=math.pow(THETA, -n / 64.0), scalar2=None, op0=ALU.mult,
-            )
-        nc.vector.tensor_copy(out=freq[:, 64:128], in_=freq[:, 0:64])
-        carried = const.tile([P, ROPE // 2, 2], F32)
-        freq_pairs = freq[:].rearrange("p (m e) -> p m e", e=2)
-        nc.vector.tensor_copy(out=carried[:, :, 0], in_=freq_pairs[:, :, 1])
-        nc.vector.tensor_scalar(
-            out=carried[:, :, 1], in0=freq_pairs[:, :, 0], scalar1=-1.0, scalar2=None, op0=ALU.mult
-        )
-        position = const.tile([P, TOK], I32)
-        nc.gpsimd.iota(position[:], pattern=[[1, TOK]], base=0, channel_multiplier=TOK)
-        turns = const.tile([P, TOK], F32)
-        nc.vector.tensor_scalar(
-            out=turns[:], in0=position[:], scalar1=1.0 / (2.0 * math.pi), scalar2=None, op0=ALU.mult
-        )
-        angle = const.tile([P, 2, TOK, ROPE], F32)
-        for j in range(TOK):
-            nc.vector.tensor_scalar(
-                out=angle[:, 0, j, :], in0=freq[:],
-                scalar1=turns[:, j : j + 1], scalar2=0.25, op0=ALU.mult, op1=ALU.add,
-            )
-            nc.vector.tensor_scalar(
-                out=angle[:, 1, j, :], in0=carried[:].rearrange("p m e -> p (m e)"),
-                scalar1=turns[:, j : j + 1], scalar2=None, op0=ALU.mult,
-            )
-        angle_flat = angle[:].rearrange("p c j f -> p (c j f)")
-        shifted = const.tile([P, 2 * TOK * ROPE], F32)
-        nc.vector.tensor_scalar(
-            out=shifted[:], in0=angle_flat, scalar1=ROUND_MAGIC, scalar2=None, op0=ALU.add
-        )
-        minus_frac = const.tile([P, 2 * TOK * ROPE], F32)
-        nc.vector.scalar_tensor_tensor(
-            out=minus_frac[:], in0=shifted[:], scalar=ROUND_MAGIC, in1=angle_flat,
-            op0=ALU.subtract, op1=ALU.subtract,
-        )
-        tab = const.tile([P, 2, TOK * ROPE], F32)
-        warm = const.tile([P, 2], F32)
+            def new_x(b, j):
+                grouped = xq.tile([P, GROUPS, P, PACK], BF16, align_bytes=64)
+                codes = xq.tile([P, GROUPS * P], U32, align_bytes=64)
+                scales = xq.tile([P, GROUPS * P], U8, align_bytes=64)
+                return b, j, grouped, codes, scales
 
-        def quantise_x(b, j, bank_pool, bank_tag, warm_bank=None):
-            x_words = x_sb[b][:].bitcast(F32)
-            grouped = xq.tile([P, GROUPS, P, PACK], BF16, align_bytes=64)
-            grouped_words = grouped[:].bitcast(F32)
-            codes = xq.tile([P, GROUPS * P], U32, align_bytes=64)
-            scales = xq.tile([P, GROUPS * P], U8, align_bytes=64)
-            for half in range(GROUPS // 2):
-                xt = bank_pool.tile([P, 2, 2, P], F32, tag=bank_tag, name="xt")
+            def turn_x(x_mx, half, pool, tag):
+                b, j = x_mx[0], x_mx[1]
+                x_words = x_sb[b][:].bitcast(F32)
+                xt = pool.tile([P, 2, 2, P], F32, tag=tag, name="xt")
                 for gi in range(2):
                     g = 2 * half + gi
                     for u in range(2):
@@ -188,130 +204,125 @@ def tile_multiheadlatentattention_pb_kernel(
                             in_=x_words[:, j, 256 * g + u : 256 * (g + 1) : 2],
                             identity=ident[:],
                         )
-                copy = nc.vector.tensor_copy if half == 0 else nc.scalar.copy
+                return xt
+
+            def copy_x(x_mx, half, xt, copy):
                 copy(
-                    out=grouped_words[:, 2 * half : 2 * half + 2, :, :],
+                    out=x_mx[2][:].bitcast(F32)[:, 2 * half : 2 * half + 2, :, :],
                     in_=xt[:].rearrange("p g u k -> p g k u"),
                 )
+
+            def quantise_x(x_mx, half):
+                grouped, codes, scales = x_mx[2], x_mx[3], x_mx[4]
                 cols = slice(2 * half * P, 2 * (half + 1) * P)
                 nc.vector.quantize_mx(
                     out=codes[:, cols].bitcast(FP8X4),
                     scales=scales[:, cols],
                     in_=grouped[:, 2 * half : 2 * half + 2, :, :].rearrange("p g k t -> p (g k t)"),
                 )
-            if warm_bank is not None:
-                keep_warm(grouped[:, 0, :, :].rearrange("p k t -> p (k t)"), WARM_BETWEEN, warm_bank)
-            return codes, scales
 
-        def first_pass(x_mx_j, g, n_cols, acc):
-            codes, scales = x_mx_j
-            nc.tensor.matmul_mx(
-                out=acc,
-                lhsT=codes[:, g * P : (g + 1) * P].bitcast(FP8X4),
-                lhsT_scale=scales[:, g * P : (g + 1) * P],
-                rhs=wa_words[:, g, n_cols].bitcast(FP8X4),
-                rhs_scale=wa_planes[4 * g : P, n_cols],
-                start=(g == 0),
-                stop=(g == GROUPS - 1),
-            )
+            def first_pass(x_mx, g, n_cols, acc):
+                codes, scales = x_mx[3], x_mx[4]
+                nc.tensor.matmul_mx(
+                    out=acc,
+                    lhsT=codes[:, g * P : (g + 1) * P].bitcast(FP8X4),
+                    lhsT_scale=scales[:, g * P : (g + 1) * P],
+                    rhs=wa_words[:, g, n_cols].bitcast(FP8X4),
+                    rhs_scale=wa_planes[4 * g : P, n_cols],
+                    start=(g == 0),
+                    stop=(g == GROUPS - 1),
+                )
 
-        def first_matmul(x_mx):
-            latent = []
-            for j in range(TOK):
-                latent_j = lat_ps.tile([P, LATENT], F32, name="latent_j")
-                latent.append(latent_j)
-            for g in range(GROUPS):
+            def new_latent():
+                latent = []
                 for j in range(TOK):
-                    first_pass(x_mx[j], g, slice(0, LATENT), latent[j][:])
-            r_bank = rope_ps.tile([P, 512], F32, tag="rope")
-            for j in range(TOK):
-                for g in range(GROUPS):
-                    first_pass(x_mx[j], g, slice(LATENT, A_COLS), r_bank[:, j * ROPE : (j + 1) * ROPE])
-            return latent, r_bank
+                    latent_j = lat_ps.tile([P, LATENT], F32, name="latent_j")
+                    latent.append(latent_j)
+                return latent
 
-        def quantise_h(latent, warm_bank=None):
-            rms = []
-            for j in range(TOK):
+            def latent_passes(x_mx, latent, groups):
+                for g in groups:
+                    for j in range(TOK):
+                        first_pass(x_mx[j], g, slice(0, LATENT), latent[j][:])
+
+            def rope_passes(x_mx):
+                bank = rope_ps.tile([P, 512], F32, tag="rope")
+                for j in range(TOK):
+                    for g in range(GROUPS):
+                        first_pass(x_mx[j], g, slice(LATENT, A_COLS), bank[:, j * ROPE : (j + 1) * ROPE])
+                return bank
+
+            def reciprocal_rms(latent, j):
                 squares = norm.tile([P, LATENT], BF16)
                 mean_sq = norm.tile([P, 1], F32)
                 nc.scalar.activation(
                     out=squares[:], in_=latent[j][:], func=ACT.Square,
                     scale=1.0 / math.sqrt(LATENT), accum_out=mean_sq[:],
                 )
-                rms_j = norm.tile([P, 1], F32, name="rms_j")
-                nc.scalar.activation(out=rms_j[:], in_=mean_sq[:], func=ACT.Sqrt, bias=EPS, scale=1.0)
-                rms.append(rms_j)
-                if warm_bank is not None:
-                    keep_warm(squares[:], WARM_NORM, warm_bank)
-            normed = []
-            for j in range(TOK):
                 rstd = norm.tile([P, 1], F32)
-                nc.vector.reciprocal(out=rstd[:], in_=rms[j][:])
-                normed_j = norm.tile([P, PACK, P], F32, name="normed_j")
-                nc.vector.tensor_scalar(
-                    out=normed_j[:], in0=latent[j][:].rearrange("p (q t) -> p t q", t=PACK),
-                    scalar1=rstd[:, 0:1], scalar2=None, op0=ALU.mult,
+                nc.scalar.activation(
+                    out=rstd[:], in_=mean_sq[:], func=ACT.Abs_reciprocal_sqrt, bias=EPS, scale=1.0
                 )
-                normed.append(normed_j)
-            normed_t = []
-            for j in range(TOK):
-                normed_t_j = tp_ps.tile([P, PACK, P], F32, tag="tp", name="normed_t_j")
-                for t in range(PACK):
-                    nc.tensor.transpose(out=normed_t_j[:, t, :], in_=normed[j][:, t, :], identity=ident[:])
-                normed_t.append(normed_t_j)
-            h_grouped = []
-            for j in range(TOK):
-                h_grouped_j = norm.tile([P, P, PACK], BF16, align_bytes=64, name="h_grouped_j")
-                nc.vector.tensor_tensor(
-                    out=h_grouped_j[:], in0=normed_t[j][:].rearrange("p t k -> p k t"),
-                    in1=gain[:].unsqueeze(1).to_broadcast([P, P, PACK]), op=ALU.mult,
+                return rstd
+
+            def normalise(normed, latent, j, rstd, planes):
+                nc.vector.scalar_tensor_tensor(
+                    out=normed[:, planes, :],
+                    in0=latent[j][:].rearrange("p (q t) -> p t q", t=PACK)[:, planes, :],
+                    scalar=rstd[:, 0:1], in1=gain[:, planes, :], op0=ALU.mult, op1=ALU.mult,
                 )
-                h_grouped.append(h_grouped_j)
-                if warm_bank is not None and j == 0:
-                    keep_warm(h_grouped_j[:].rearrange("p k t -> p (k t)"), WARM_NORM, warm_bank)
-            h_mx = []
-            for j in range(TOK):
+
+            def turn_h(turned, normed, planes):
+                for i, t in enumerate(range(planes.start, planes.stop)):
+                    nc.tensor.transpose(out=turned[:, i, :], in_=normed[:, t, :], identity=ident[:])
+
+            def round_h(h_grouped, turned, planes, copy):
+                copy(
+                    out=h_grouped[:, :, planes],
+                    in_=turned[:, 0 : planes.stop - planes.start, :].rearrange("p t k -> p k t"),
+                )
+
+            def quantise_h(h_grouped):
                 codes = norm.tile([P, P], U32, align_bytes=64)
                 scales = norm.tile([P, P], U8, align_bytes=64)
                 nc.vector.quantize_mx(
                     out=codes[:].bitcast(FP8X4),
                     scales=scales[:],
-                    in_=h_grouped[j][:].rearrange("p k t -> p (k t)"),
+                    in_=h_grouped[:].rearrange("p k t -> p (k t)"),
                 )
-                h_mx.append((codes, scales))
-            return h_mx
+                return codes, scales
 
-        def rotate(r_bank):
-            prod = rope.tile([P, 2, TOK * ROPE], F32)
-            nc.vector.tensor_tensor(
-                out=prod[:], in0=r_bank.unsqueeze(1).to_broadcast([P, 2, TOK * ROPE]),
-                in1=tab[:], op=ALU.mult,
-            )
-            own = prod[:, 0, :].rearrange("p (m e) -> p m e", e=2)
-            carry = prod[:, 1, :].rearrange("p (m e) -> p m e", e=2)
-            rotated = rope.tile([P, TOK, ROPE], F32)
-            rotated_pairs = rotated[:].rearrange("p j (m e) -> p (j m) e", e=2)
-            for e in range(2):
-                nc.gpsimd.tensor_tensor(
-                    out=rotated_pairs[:, :, e], in0=own[:, :, e], in1=carry[:, :, 1 - e], op=ALU.add
-                )
-            return rotated
+            def rotate(r_bank):
+                prod = rope.tile([P, 2, TOK * ROPE], F32)
+                for c in range(2):
+                    nc.vector.tensor_tensor(
+                        out=prod[:, c, :].rearrange("p (j r f) -> p j r f", j=TOK, f=HALF),
+                        in0=r_bank[:, 0 : TOK * ROPE].rearrange("p (j r f) -> p j r f", j=TOK, f=HALF),
+                        in1=tab[:, c, :, :].unsqueeze(2).to_broadcast([P, TOK, 2, HALF]), op=ALU.mult,
+                    )
+                own = prod[:, 0, :].rearrange("p (m e) -> p m e", e=2)
+                carry = prod[:, 1, :].rearrange("p (m e) -> p m e", e=2)
+                rotated = rope.tile([P, TOK, ROPE], F32)
+                rotated_pairs = rotated[:].rearrange("p j (m e) -> p (j m) e", e=2)
+                for e in range(2):
+                    nc.gpsimd.tensor_tensor(
+                        out=rotated_pairs[:, :, e], in0=own[:, :, e], in1=carry[:, :, 1 - e], op=ALU.add
+                    )
+                return rotated
 
-        def spread_rope(rotated, k_rows):
-            for pair in range(N_PAIRS):
-                heads = slice(PAIR * pair, PAIR * (pair + 1))
-                nc.gpsimd.tensor_scalar(
-                    out=k_rows[:, heads, :, NOPE:K_OUT],
-                    in0=rotated[:].unsqueeze(1).to_broadcast([P, PAIR, TOK, ROPE]),
-                    scalar1=1.0, scalar2=0.0, op0=ALU.mult, op1=ALU.add,
-                )
+            def spread_rope(rotated, k_rows):
+                for pair in range(N_PAIRS):
+                    heads = slice(PAIR * pair, PAIR * (pair + 1))
+                    nc.gpsimd.tensor_scalar(
+                        out=k_rows[:, heads, :, NOPE:K_OUT],
+                        in0=rotated[:].unsqueeze(1).to_broadcast([P, PAIR, TOK, ROPE]),
+                        scalar1=1.0, scalar2=0.0, op0=ALU.mult, op1=ALU.add,
+                    )
 
-        def second_matmul(b, pair, h_mx, k_sb, v_sb):
-            heads = slice(PAIR * pair, PAIR * (pair + 1))
-            plane = (pair * PAIR_COLS) // B_PLANE_COLS
-            in_plane = (pair * PAIR_COLS) % B_PLANE_COLS
-            for j in range(TOK):
-                codes, scales = h_mx[j]
+            def second_matmul(pair, j, h_mx_j):
+                plane = (pair * PAIR_COLS) // B_PLANE_COLS
+                in_plane = (pair * PAIR_COLS) % B_PLANE_COLS
+                codes, scales = h_mx_j
                 kv = kv_ps.tile([P, 512], F32, tag="kv")
                 for lo, hi in ((0, 256), (256, PAIR_COLS)):
                     nc.tensor.matmul_mx(
@@ -323,68 +334,153 @@ def tile_multiheadlatentattention_pb_kernel(
                         start=True,
                         stop=True,
                     )
+                return kv
+
+            def copy_kv(b, pair, j, kv, copy):
+                heads = slice(PAIR * pair, PAIR * (pair + 1))
                 by_head = kv[:, 0:PAIR_COLS].rearrange("p (h c) -> p h c", h=PAIR)
-                copy = nc.vector.tensor_copy if j == 0 else nc.scalar.copy
-                copy(out=v_sb[:, heads, j, :], in_=by_head[:, :, NOPE:HEAD_COLS])
-                copy(out=k_sb[:, heads, j, 0:NOPE], in_=by_head[:, :, 0:NOPE])
-            nc.sync.dma_start(
-                out=out_1[b, heads].rearrange("h (p j) d -> p h (j d)", j=TOK),
-                in_=v_sb[:, heads, :, :].rearrange("p h j d -> p h (j d)"),
-            )
+                copy(out=v_sb[b][:, heads, j, :], in_=by_head[:, :, NOPE:HEAD_COLS])
+                copy(out=k_sb[b][:, heads, j, 0:NOPE], in_=by_head[:, :, 0:NOPE])
 
-        def store_k(b, pair, k_sb):
-            heads = slice(PAIR * pair, PAIR * (pair + 1))
-            nc.sync.dma_start(
-                out=out_0[b, heads].rearrange("h (p j) d -> p h (j d)", j=TOK),
-                in_=k_sb[:, heads, :, :].rearrange("p h j d -> p h (j d)"),
-            )
+            def store_v(b, pair):
+                heads = slice(PAIR * pair, PAIR * (pair + 1))
+                nc.sync.dma_start(
+                    out=out_1[b, heads].rearrange("h (p j) d -> p h (j d)", j=TOK),
+                    in_=v_sb[b][:, heads, :, :].rearrange("p h j d -> p h (j d)"),
+                )
 
-        k_sb = []
-        v_sb = []
-        for b in range(BATCH):
-            k_b = outs.tile([P, HEADS, TOK, K_OUT], F32, name="k_b")
-            v_b = outs.tile([P, HEADS, TOK, VDIM], F32, name="v_b")
-            k_sb.append(k_b)
-            v_sb.append(v_b)
+            def store_k(b, pair):
+                heads = slice(PAIR * pair, PAIR * (pair + 1))
+                nc.sync.dma_start(
+                    out=out_0[b, heads].rearrange("h (p j) d -> p h (j d)", j=TOK),
+                    in_=k_sb[b][:, heads, :, :].rearrange("p h j d -> p h (j d)"),
+                )
 
-        with tc.manual_schedule(engines={mybir.EngineType.Activation}):
-            nc.scalar.activation(out=warm[:, 0:1], in_=turns[:, 0:1], func=ACT.Sqrt, bias=1.0, scale=0.0)
-            warm_first = rope_ps.tile([P, 512], F32, tag="rope")
-            keep_warm(zeros[:], WARM_START, warm_first[:])
-            x_mx = [quantise_x(0, 0, tp_ps, "tp", warm_first[:]), quantise_x(0, 1, kv_ps, "kv")]
-            latent, r_bank = first_matmul(x_mx)
-            warm_later = kv_ps.tile([P, 512], F32, tag="kv")
-            h_mx = quantise_h(latent, warm_later[:])
+            def multiply_pair(pair, h_mx):
+                return [second_matmul(pair, j, h_mx[j]) for j in range(TOK)]
+
+            def finish_pair(b, pair, kv, copies):
+                for j in range(TOK):
+                    copy_kv(b, pair, j, kv[j], copies[j])
+                store_v(b, pair)
+                store_k(b, pair)
+
+            k_sb = []
+            v_sb = []
+            for b in range(BATCH):
+                k_b = outs.tile([P, HEADS, TOK, K_OUT], F32, name="k_b")
+                v_b = outs.tile([P, HEADS, TOK, VDIM], F32, name="v_b")
+                k_sb.append(k_b)
+                v_sb.append(v_b)
+
+            v_copy, s_copy = nc.vector.tensor_copy, nc.scalar.copy
+            both = (v_copy, s_copy)
+            x_mx = [new_x(0, 0), new_x(0, 1)]
+            warm_bank = rope_ps.tile([P, 512], F32, tag="rope")
+            keep_warm(zeros[:], WARM_START, warm_bank[:])
+            xt = [turn_x(x_mx[0], 0, tp_ps, "tp"), turn_x(x_mx[0], 1, tp_ps, "tp")]
+            gain_bank = kv_ps.tile([P, 512], F32, tag="kv")
+            copy_x(x_mx[0], 0, xt[0], v_copy)
+            copy_x(x_mx[0], 1, xt[1], s_copy)
+            xt = [turn_x(x_mx[1], 0, kv_ps, "kv"), turn_x(x_mx[1], 1, kv_ps, "kv")]
+            quantise_x(x_mx[0], 0)
+            copy_x(x_mx[1], 0, xt[0], v_copy)
+            quantise_x(x_mx[0], 1)
+            copy_x(x_mx[1], 1, xt[1], s_copy)
+            nc.tensor.matmul(out=gain_bank[:], lhsT=ones[:], rhs=gain_row[:], start=True, stop=True)
+            quantise_x(x_mx[1], 0)
+            gain = const.tile([P, PACK, P], F32)
+            nc.scalar.copy(out=gain[:], in_=gain_bank[:].rearrange("p (q t) -> p t q", t=PACK))
             nc.scalar.activation(
-                out=tab[:].rearrange("p c f -> p (c f)"), in_=minus_frac[:], func=ACT.Sin,
-                scale=-2.0 * math.pi,
+                out=warm[:, 1:2], in_=gain[:, 0, 0:1], func=ACT.Abs_reciprocal_sqrt, bias=1.0, scale=0.0
             )
-            nc.scalar.activation(out=warm[:, 1:2], in_=tab[:, 0, 0:1], func=ACT.Sqrt, bias=1.0, scale=0.0)
+            quantise_x(x_mx[1], 1)
+            latent = new_latent()
+            latent_passes(x_mx, latent, range(GROUPS))
+            r_bank = rope_passes(x_mx)
 
-        second_matmul(0, 0, h_mx, k_sb[0], v_sb[0])
-        second_matmul(0, 1, h_mx, k_sb[0], v_sb[0])
-        rotated = rotate(r_bank[:, 0 : TOK * ROPE])
-        spread_rope(rotated, k_sb[0])
-        x_mx_1 = [quantise_x(1, 0, tp_ps, "tp")]
-        second_matmul(0, 2, h_mx, k_sb[0], v_sb[0])
-        x_mx_1.append(quantise_x(1, 1, tp_ps, "tp"))
-        second_matmul(0, 3, h_mx, k_sb[0], v_sb[0])
-        store_k(0, 0, k_sb[0])
-        latent_1, r_bank_1 = first_matmul(x_mx_1)
-        second_matmul(0, 4, h_mx, k_sb[0], v_sb[0])
-        store_k(0, 1, k_sb[0])
-        h_mx_1 = quantise_h(latent_1)
-        second_matmul(0, 5, h_mx, k_sb[0], v_sb[0])
-        store_k(0, 2, k_sb[0])
-        rotated_1 = rotate(r_bank_1[:, 0 : TOK * ROPE])
-        spread_rope(rotated_1, k_sb[1])
-        second_matmul(0, 6, h_mx, k_sb[0], v_sb[0])
-        store_k(0, 3, k_sb[0])
-        second_matmul(0, 7, h_mx, k_sb[0], v_sb[0])
-        store_k(0, 4, k_sb[0])
-        store_k(0, 5, k_sb[0])
-        store_k(0, 6, k_sb[0])
-        store_k(0, 7, k_sb[0])
-        for pair in range(N_PAIRS):
-            second_matmul(1, pair, h_mx_1, k_sb[1], v_sb[1])
-            store_k(1, pair, k_sb[1])
+            def norm_head(latent, between, fill):
+                whole, halves = slice(0, PACK), (slice(0, PACK // 2), slice(PACK // 2, PACK))
+                normed_0 = norm.tile([P, PACK, P], F32, tag="normed")
+                normed_1 = norm.tile([P, PACK, P], F32, tag="normed")
+                h_0 = norm.tile([P, P, PACK], BF16, align_bytes=64, tag="h")
+                h_1 = norm.tile([P, P, PACK], BF16, align_bytes=64, tag="h")
+                rstd_0 = reciprocal_rms(latent, 0)
+                normalise(normed_0, latent, 0, rstd_0, whole)
+                rstd_1 = reciprocal_rms(latent, 1)
+                between()
+                turned_0 = tp_ps.tile([P, PACK, P], F32, tag="tp")
+                turn_h(turned_0, normed_0, whole)
+                for half, pool, tag in zip(halves, (tp_ps, kv_ps), ("tp", "kv")):
+                    normalise(normed_1, latent, 1, rstd_1, half)
+                    turned_1 = pool.tile([P, PACK, P], F32, tag=tag)
+                    turn_h(turned_1, normed_1, half)
+                    round_h(h_1, turned_1, half, s_copy)
+                round_h(h_0, turned_0, whole, v_copy)
+                q_0 = quantise_h(h_0)
+                fill()
+                q_1 = quantise_h(h_1)
+                return [q_0, q_1]
+
+            x_mx_1 = [new_x(1, 0), new_x(1, 1)]
+            rotated = []
+            x_banks = []
+
+            def fill_head():
+                rotated.append(rotate(r_bank))
+                x_banks.append(turn_x(x_mx_1[0], 0, tp_ps, "tp"))
+
+            def warm_head():
+                warm_bank = kv_ps.tile([P, 512], F32, tag="kv")
+                keep_warm(zeros[:], WARM_NORM, warm_bank[:])
+
+            h_mx = norm_head(latent, warm_head, fill_head)
+
+            kv_00 = second_matmul(0, 0, h_mx[0])
+            kv_10 = second_matmul(1, 0, h_mx[0])
+            copy_kv(0, 0, 0, kv_00, s_copy)
+            kv_01 = second_matmul(0, 1, h_mx[1])
+            copy_kv(0, 1, 0, kv_10, s_copy)
+            kv_11 = second_matmul(1, 1, h_mx[1])
+            copy_kv(0, 0, 1, kv_01, v_copy)
+            store_v(0, 0)
+            copy_kv(0, 1, 1, kv_11, s_copy)
+            store_v(0, 1)
+
+            spread_rope(rotated[0], k_sb[0])
+            store_k(0, 0)
+            store_k(0, 1)
+            x_bank = turn_x(x_mx_1[0], 1, tp_ps, "tp")
+            copy_x(x_mx_1[0], 0, x_banks[0], v_copy)
+            copy_x(x_mx_1[0], 1, x_bank, s_copy)
+            quantise_x(x_mx_1[0], 0)
+            kv = multiply_pair(2, h_mx)
+            x_bank = turn_x(x_mx_1[1], 0, tp_ps, "tp")
+            finish_pair(0, 2, kv, both)
+            quantise_x(x_mx_1[0], 1)
+            copy_x(x_mx_1[1], 0, x_bank, v_copy)
+            copy_x(x_mx_1[1], 1, turn_x(x_mx_1[1], 1, tp_ps, "tp"), s_copy)
+            quantise_x(x_mx_1[1], 0)
+            kv = multiply_pair(3, h_mx)
+            latent_1 = new_latent()
+            quantise_x(x_mx_1[1], 1)
+            latent_passes(x_mx_1, latent_1, range(0, 2))
+            finish_pair(0, 3, kv, both)
+            kv = multiply_pair(4, h_mx)
+            latent_passes(x_mx_1, latent_1, range(2, GROUPS))
+            finish_pair(0, 4, kv, both)
+            kv = multiply_pair(5, h_mx)
+            r_bank_1 = rope_passes(x_mx_1)
+            finish_pair(0, 5, kv, (v_copy, v_copy))
+
+            def fill_second():
+                rotated.append(rotate(r_bank_1))
+                finish_pair(0, 7, multiply_pair(7, h_mx), both)
+
+            def between_second():
+                finish_pair(0, 6, multiply_pair(6, h_mx), (s_copy, s_copy))
+
+            h_mx_1 = norm_head(latent_1, between_second, fill_second)
+            spread_rope(rotated[1], k_sb[1])
+            for pair in range(N_PAIRS):
+                finish_pair(1, pair, multiply_pair(pair, h_mx_1), both)

@@ -38,7 +38,7 @@ PLANES = 4
 B_PLANE_COLS = B_COLS // PLANES
 
 
-WARM_START = 5
+WARM_START = 4
 WARM_NORM = 1
 
 ROUND_MAGIC = 1.5 * 2.0**23
@@ -240,9 +240,9 @@ def tile_multiheadlatentattention_pb_kernel(
                     latent.append(latent_j)
                 return latent
 
-            def latent_passes(x_mx, latent, groups):
+            def latent_passes(x_mx, latent, groups, tiles=range(TOK)):
                 for g in groups:
-                    for j in range(TOK):
+                    for j in tiles:
                         first_pass(x_mx[j], g, slice(0, LATENT), latent[j][:])
 
             def rope_passes(x_mx):
@@ -384,22 +384,26 @@ def tile_multiheadlatentattention_pb_kernel(
             copy_x(x_mx[0], 1, xt[1], s_copy)
             xt = [turn_x(x_mx[1], 0, kv_ps, "kv"), turn_x(x_mx[1], 1, kv_ps, "kv")]
             quantise_x(x_mx[0], 0)
-            copy_x(x_mx[1], 0, xt[0], v_copy)
+            copy_x(x_mx[1], 0, xt[0], s_copy)
             quantise_x(x_mx[0], 1)
-            copy_x(x_mx[1], 1, xt[1], s_copy)
+            copy_x(x_mx[1], 1, xt[1], v_copy)
+            latent = new_latent()
+            latent_passes(x_mx, latent, range(0, 1), tiles=(0,))
             nc.tensor.matmul(out=gain_bank[:], lhsT=ones[:], rhs=gain_row[:], start=True, stop=True)
+            latent_passes(x_mx, latent, range(1, 2), tiles=(0,))
             quantise_x(x_mx[1], 0)
             gain = const.tile([P, PACK, P], F32)
-            nc.scalar.copy(out=gain[:], in_=gain_bank[:].rearrange("p (q t) -> p t q", t=PACK))
             nc.scalar.activation(
-                out=warm[:, 1:2], in_=gain[:, 0, 0:1], func=ACT.Abs_reciprocal_sqrt, bias=1.0, scale=0.0
+                out=warm[:, 1:2], in_=tab[:, 0, 0, 0:1], func=ACT.Abs_reciprocal_sqrt, bias=1.0, scale=0.0
             )
+            nc.scalar.copy(out=gain[:], in_=gain_bank[:].rearrange("p (q t) -> p t q", t=PACK))
             quantise_x(x_mx[1], 1)
-            latent = new_latent()
-            latent_passes(x_mx, latent, range(GROUPS))
+            latent_passes(x_mx, latent, range(0, 2), tiles=(1,))
+            for j in range(TOK):
+                latent_passes(x_mx, latent, range(2, GROUPS), tiles=(j,))
             r_bank = rope_passes(x_mx)
 
-            def norm_head(latent, between, fill):
+            def norm_head(latent, between):
                 whole, halves = slice(0, PACK), (slice(0, PACK // 2), slice(PACK // 2, PACK))
                 normed_0 = norm.tile([P, PACK, P], F32, tag="normed")
                 normed_1 = norm.tile([P, PACK, P], F32, tag="normed")
@@ -418,41 +422,35 @@ def tile_multiheadlatentattention_pb_kernel(
                     round_h(h_1, turned_1, half, s_copy)
                 round_h(h_0, turned_0, whole, v_copy)
                 q_0 = quantise_h(h_0)
-                fill()
                 q_1 = quantise_h(h_1)
                 return [q_0, q_1]
 
             x_mx_1 = [new_x(1, 0), new_x(1, 1)]
-            rotated = []
-            x_banks = []
-
-            def fill_head():
-                rotated.append(rotate(r_bank))
-                x_banks.append(turn_x(x_mx_1[0], 0, tp_ps, "tp"))
-
             def warm_head():
                 warm_bank = kv_ps.tile([P, 512], F32, tag="kv")
                 keep_warm(zeros[:], WARM_NORM, warm_bank[:])
 
-            h_mx = norm_head(latent, warm_head, fill_head)
+            h_mx = norm_head(latent, warm_head)
+            rotated = rotate(r_bank)
 
             kv_00 = second_matmul(0, 0, h_mx[0])
             kv_10 = second_matmul(1, 0, h_mx[0])
             copy_kv(0, 0, 0, kv_00, s_copy)
             kv_01 = second_matmul(0, 1, h_mx[1])
             copy_kv(0, 1, 0, kv_10, s_copy)
+            x_bank = turn_x(x_mx_1[0], 0, tp_ps, "tp")
             kv_11 = second_matmul(1, 1, h_mx[1])
             copy_kv(0, 0, 1, kv_01, v_copy)
             store_v(0, 0)
             copy_kv(0, 1, 1, kv_11, s_copy)
             store_v(0, 1)
 
-            spread_rope(rotated[0], k_sb[0])
+            spread_rope(rotated, k_sb[0])
             store_k(0, 0)
             store_k(0, 1)
-            x_bank = turn_x(x_mx_1[0], 1, tp_ps, "tp")
-            copy_x(x_mx_1[0], 0, x_banks[0], v_copy)
-            copy_x(x_mx_1[0], 1, x_bank, s_copy)
+            x_bank_1 = turn_x(x_mx_1[0], 1, tp_ps, "tp")
+            copy_x(x_mx_1[0], 0, x_bank, v_copy)
+            copy_x(x_mx_1[0], 1, x_bank_1, s_copy)
             quantise_x(x_mx_1[0], 0)
             kv = multiply_pair(2, h_mx)
             x_bank = turn_x(x_mx_1[1], 0, tp_ps, "tp")
@@ -473,14 +471,12 @@ def tile_multiheadlatentattention_pb_kernel(
             r_bank_1 = rope_passes(x_mx_1)
             finish_pair(0, 5, kv, (v_copy, v_copy))
 
-            def fill_second():
-                rotated.append(rotate(r_bank_1))
-                finish_pair(0, 7, multiply_pair(7, h_mx), both)
-
             def between_second():
                 finish_pair(0, 6, multiply_pair(6, h_mx), (s_copy, s_copy))
 
-            h_mx_1 = norm_head(latent_1, between_second, fill_second)
-            spread_rope(rotated[1], k_sb[1])
+            h_mx_1 = norm_head(latent_1, between_second)
+            rotated_1 = rotate(r_bank_1)
+            spread_rope(rotated_1, k_sb[1])
+            finish_pair(0, 7, multiply_pair(7, h_mx), (s_copy, s_copy))
             for pair in range(N_PAIRS):
                 finish_pair(1, pair, multiply_pair(pair, h_mx_1), both)

@@ -39,6 +39,7 @@ B_PLANE_COLS = B_COLS // PLANES
 
 
 WARM_START = 4
+WARM_TURN = 1
 WARM_NORM = 1
 
 ROUND_MAGIC = 1.5 * 2.0**23
@@ -80,6 +81,7 @@ def tile_multiheadlatentattention_pb_kernel(
             make_identity(nc, ident[:])
             gain_row = const.tile([P, LATENT], BF16)
             nc.gpsimd.memset(gain_row[:].bitcast(F32), 0.0)
+            nc.gpsimd.dma_start(out=gain_row[0:1, :], in_=kv_a_norm_w.rearrange("(o n) -> o n", o=1))
             nc.gpsimd.memset(wb_planes[:].bitcast(F32), 0.0)
 
             wa_words = const.tile([P, GROUPS, A_COLS], U32, align_bytes=64)
@@ -99,20 +101,18 @@ def tile_multiheadlatentattention_pb_kernel(
                     )
 
             load_x(0, 0, pieces=2)
+            load_x(0, 1, pieces=2)
             for quad in range(QUADS):
                 nc.sync.dma_start(
                     out=wa_planes[32 * quad : 32 * quad + 16, :].bitcast(I32),
                     in_=Wkva_scales[:, 4 * quad : 4 * quad + 4, :].bitcast(I32),
                 )
-            load_x(0, 1, pieces=2)
             wa_dram = Wkva_words.rearrange("g p n t -> p g (n t)")
             for g in range(GROUPS):
                 nc.sync.dma_start(
                     out=wa_words[:, g, 0:LATENT].bitcast(I32),
                     in_=wa_dram[:, g, 0 : PACK * LATENT].bitcast(I32),
                 )
-                if g == 0:
-                    nc.sync.dma_start(out=gain_row[0:1, :], in_=kv_a_norm_w.rearrange("(o n) -> o n", o=1))
             nc.sync.dma_start(
                 out=wa_words[:, :, LATENT:A_COLS].bitcast(I32),
                 in_=wa_dram[:, :, PACK * LATENT : PACK * A_COLS].bitcast(I32),
@@ -382,7 +382,9 @@ def tile_multiheadlatentattention_pb_kernel(
             gain_bank = kv_ps.tile([P, 512], F32, tag="kv")
             copy_x(x_mx[0], 0, xt[0], v_copy)
             copy_x(x_mx[0], 1, xt[1], s_copy)
+            keep_warm(zeros[:], WARM_TURN, warm_bank[:])
             xt = [turn_x(x_mx[1], 0, kv_ps, "kv"), turn_x(x_mx[1], 1, kv_ps, "kv")]
+            keep_warm(zeros[:], WARM_TURN, warm_bank[:])
             quantise_x(x_mx[0], 0)
             copy_x(x_mx[1], 0, xt[0], s_copy)
             quantise_x(x_mx[0], 1)
@@ -390,20 +392,20 @@ def tile_multiheadlatentattention_pb_kernel(
             latent = new_latent()
             latent_passes(x_mx, latent, range(0, 1), tiles=(0,))
             nc.tensor.matmul(out=gain_bank[:], lhsT=ones[:], rhs=gain_row[:], start=True, stop=True)
+            gain = const.tile([P, PACK, P], F32)
             latent_passes(x_mx, latent, range(1, 2), tiles=(0,))
             quantise_x(x_mx[1], 0)
-            gain = const.tile([P, PACK, P], F32)
             nc.scalar.activation(
                 out=warm[:, 1:2], in_=tab[:, 0, 0, 0:1], func=ACT.Abs_reciprocal_sqrt, bias=1.0, scale=0.0
             )
-            nc.scalar.copy(out=gain[:], in_=gain_bank[:].rearrange("p (q t) -> p t q", t=PACK))
             quantise_x(x_mx[1], 1)
+            v_copy(out=gain[:], in_=gain_bank[:].rearrange("p (q t) -> p t q", t=PACK))
             latent_passes(x_mx, latent, range(0, 2), tiles=(1,))
             for j in range(TOK):
                 latent_passes(x_mx, latent, range(2, GROUPS), tiles=(j,))
             r_bank = rope_passes(x_mx)
 
-            def norm_head(latent, between):
+            def norm_head(latent, between, behind):
                 whole, halves = slice(0, PACK), (slice(0, PACK // 2), slice(PACK // 2, PACK))
                 normed_0 = norm.tile([P, PACK, P], F32, tag="normed")
                 normed_1 = norm.tile([P, PACK, P], F32, tag="normed")
@@ -420,6 +422,7 @@ def tile_multiheadlatentattention_pb_kernel(
                     turned_1 = pool.tile([P, PACK, P], F32, tag=tag)
                     turn_h(turned_1, normed_1, half)
                     round_h(h_1, turned_1, half, s_copy)
+                behind()
                 round_h(h_0, turned_0, whole, v_copy)
                 q_0 = quantise_h(h_0)
                 q_1 = quantise_h(h_1)
@@ -430,7 +433,7 @@ def tile_multiheadlatentattention_pb_kernel(
                 warm_bank = kv_ps.tile([P, 512], F32, tag="kv")
                 keep_warm(zeros[:], WARM_NORM, warm_bank[:])
 
-            h_mx = norm_head(latent, warm_head)
+            h_mx = norm_head(latent, warm_head, warm_head)
             rotated = rotate(r_bank)
 
             kv_00 = second_matmul(0, 0, h_mx[0])
@@ -474,7 +477,7 @@ def tile_multiheadlatentattention_pb_kernel(
             def between_second():
                 finish_pair(0, 6, multiply_pair(6, h_mx), (s_copy, s_copy))
 
-            h_mx_1 = norm_head(latent_1, between_second)
+            h_mx_1 = norm_head(latent_1, between_second, lambda: None)
             rotated_1 = rotate(r_bank_1)
             spread_rope(rotated_1, k_sb[1])
             finish_pair(0, 7, multiply_pair(7, h_mx), (s_copy, s_copy))

@@ -113,6 +113,7 @@ def tile_multiheadlatentattention_pb_kernel(
                     out=wa_words[:, g, 0:LATENT].bitcast(I32),
                     in_=wa_dram[:, g, 0 : PACK * LATENT].bitcast(I32),
                 )
+            load_x(1, 0)
             nc.sync.dma_start(
                 out=wa_words[:, :, LATENT:A_COLS].bitcast(I32),
                 in_=wa_dram[:, :, PACK * LATENT : PACK * A_COLS].bitcast(I32),
@@ -128,8 +129,8 @@ def tile_multiheadlatentattention_pb_kernel(
             for c in range(PLANES):
                 cols = slice(c * B_PLANE_COLS, (c + 1) * B_PLANE_COLS)
                 nc.sync.dma_start(out=wb_words[:, cols].bitcast(I32), in_=wb_dram[:, cols])
-                if c < TOK:
-                    load_x(1, c)
+                if c == 0:
+                    load_x(1, 1)
 
             powers = const.tile([P, 2, 8], F32)
             nc.vector.memset(powers[:, :, 0:1], 1.0)
@@ -319,11 +320,11 @@ def tile_multiheadlatentattention_pb_kernel(
                         scalar1=1.0, scalar2=0.0, op0=ALU.mult, op1=ALU.add,
                     )
 
-            def second_matmul(pair, j, h_mx_j):
+            def second_matmul(pair, j, h_mx_j, pool=kv_ps, tag="kv"):
                 plane = (pair * PAIR_COLS) // B_PLANE_COLS
                 in_plane = (pair * PAIR_COLS) % B_PLANE_COLS
                 codes, scales = h_mx_j
-                kv = kv_ps.tile([P, 512], F32, tag="kv")
+                kv = pool.tile([P, 512], F32, tag=tag, name="kv")
                 for lo, hi in ((0, 256), (256, PAIR_COLS)):
                     nc.tensor.matmul_mx(
                         out=kv[:, lo:hi],
@@ -336,21 +337,27 @@ def tile_multiheadlatentattention_pb_kernel(
                     )
                 return kv
 
-            def copy_kv(b, pair, j, kv, copy):
-                heads = slice(PAIR * pair, PAIR * (pair + 1))
-                by_head = kv[:, 0:PAIR_COLS].rearrange("p (h c) -> p h c", h=PAIR)
-                copy(out=v_sb[b][:, heads, j, :], in_=by_head[:, :, NOPE:HEAD_COLS])
-                copy(out=k_sb[b][:, heads, j, 0:NOPE], in_=by_head[:, :, 0:NOPE])
+            def heads_of(pair):
+                return slice(PAIR * pair, PAIR * (pair + 1))
+
+            def by_head(kv):
+                return kv[:, 0:PAIR_COLS].rearrange("p (h c) -> p h c", h=PAIR)
+
+            def copy_v(b, pair, j, kv, copy):
+                copy(out=v_sb[b][:, heads_of(pair), j, :], in_=by_head(kv)[:, :, NOPE:HEAD_COLS])
+
+            def copy_nope(b, pair, j, kv, copy):
+                copy(out=k_sb[b][:, heads_of(pair), j, 0:NOPE], in_=by_head(kv)[:, :, 0:NOPE])
 
             def store_v(b, pair):
-                heads = slice(PAIR * pair, PAIR * (pair + 1))
+                heads = heads_of(pair)
                 nc.sync.dma_start(
                     out=out_1[b, heads].rearrange("h (p j) d -> p h (j d)", j=TOK),
                     in_=v_sb[b][:, heads, :, :].rearrange("p h j d -> p h (j d)"),
                 )
 
             def store_k(b, pair):
-                heads = slice(PAIR * pair, PAIR * (pair + 1))
+                heads = heads_of(pair)
                 nc.sync.dma_start(
                     out=out_0[b, heads].rearrange("h (p j) d -> p h (j d)", j=TOK),
                     in_=k_sb[b][:, heads, :, :].rearrange("p h j d -> p h (j d)"),
@@ -361,8 +368,10 @@ def tile_multiheadlatentattention_pb_kernel(
 
             def finish_pair(b, pair, kv, copies):
                 for j in range(TOK):
-                    copy_kv(b, pair, j, kv[j], copies[j])
+                    copy_v(b, pair, j, kv[j], copies[j])
                 store_v(b, pair)
+                for j in range(TOK):
+                    copy_nope(b, pair, j, kv[j], copies[j])
                 store_k(b, pair)
 
             k_sb = []
@@ -403,83 +412,100 @@ def tile_multiheadlatentattention_pb_kernel(
             latent_passes(x_mx, latent, range(0, 2), tiles=(1,))
             for j in range(TOK):
                 latent_passes(x_mx, latent, range(2, GROUPS), tiles=(j,))
+            x_mx_1 = [new_x(1, 0), new_x(1, 1)]
+            x_bank_0 = turn_x(x_mx_1[0], 0, kv_ps, "kv")
             r_bank = rope_passes(x_mx)
 
-            def norm_head(latent, between, behind):
-                whole, halves = slice(0, PACK), (slice(0, PACK // 2), slice(PACK // 2, PACK))
-                normed_0 = norm.tile([P, PACK, P], F32, tag="normed")
-                normed_1 = norm.tile([P, PACK, P], F32, tag="normed")
-                h_0 = norm.tile([P, P, PACK], BF16, align_bytes=64, tag="h")
-                h_1 = norm.tile([P, P, PACK], BF16, align_bytes=64, tag="h")
-                rstd_0 = reciprocal_rms(latent, 0)
-                normalise(normed_0, latent, 0, rstd_0, whole)
-                rstd_1 = reciprocal_rms(latent, 1)
-                between()
-                turned_0 = tp_ps.tile([P, PACK, P], F32, tag="tp")
-                turn_h(turned_0, normed_0, whole)
+            whole, halves = slice(0, PACK), (slice(0, PACK // 2), slice(PACK // 2, PACK))
+
+            def new_normed():
+                normed = norm.tile([P, PACK, P], F32)
+                h_grouped = norm.tile([P, P, PACK], BF16, align_bytes=64)
+                return normed, h_grouped
+
+            def turn_first(normed):
+                turned = tp_ps.tile([P, PACK, P], F32, tag="tp")
+                turn_h(turned, normed, whole)
+                return turned
+
+            def norm_of_second(latent, rstd):
+                normed, h_grouped = new_normed()
                 for half, pool, tag in zip(halves, (tp_ps, kv_ps), ("tp", "kv")):
-                    normalise(normed_1, latent, 1, rstd_1, half)
-                    turned_1 = pool.tile([P, PACK, P], F32, tag=tag)
-                    turn_h(turned_1, normed_1, half)
-                    round_h(h_1, turned_1, half, s_copy)
-                behind()
-                round_h(h_0, turned_0, whole, v_copy)
-                q_0 = quantise_h(h_0)
-                q_1 = quantise_h(h_1)
-                return [q_0, q_1]
+                    normalise(normed, latent, 1, rstd, half)
+                    turned = pool.tile([P, PACK, P], F32, tag=tag)
+                    turn_h(turned, normed, half)
+                    round_h(h_grouped, turned, half, s_copy)
+                return h_grouped
 
-            x_mx_1 = [new_x(1, 0), new_x(1, 1)]
-            def warm_head():
-                warm_bank = kv_ps.tile([P, 512], F32, tag="kv")
-                keep_warm(zeros[:], WARM_NORM, warm_bank[:])
-
-            h_mx = norm_head(latent, warm_head, warm_head)
+            rstd_0 = reciprocal_rms(latent, 0)
+            normed_0, h_0 = new_normed()
+            normalise(normed_0, latent, 0, rstd_0, whole)
+            rstd_1 = reciprocal_rms(latent, 1)
+            copy_x(x_mx_1[0], 0, x_bank_0, s_copy)
+            warm_bank = kv_ps.tile([P, 512], F32, tag="kv")
+            keep_warm(zeros[:], WARM_NORM, warm_bank[:])
+            turned_0 = turn_first(normed_0)
+            h_1 = norm_of_second(latent, rstd_1)
+            x_bank_1 = turn_x(x_mx_1[0], 1, kv_ps, "kv")
+            round_h(h_0, turned_0, whole, v_copy)
+            copy_x(x_mx_1[0], 1, x_bank_1, s_copy)
+            h_mx = [quantise_h(h_0), quantise_h(h_1)]
             rotated = rotate(r_bank)
+            spread_rope(rotated, k_sb[0])
 
             kv_00 = second_matmul(0, 0, h_mx[0])
-            kv_10 = second_matmul(1, 0, h_mx[0])
-            copy_kv(0, 0, 0, kv_00, s_copy)
             kv_01 = second_matmul(0, 1, h_mx[1])
-            copy_kv(0, 1, 0, kv_10, s_copy)
-            x_bank = turn_x(x_mx_1[0], 0, tp_ps, "tp")
-            kv_11 = second_matmul(1, 1, h_mx[1])
-            copy_kv(0, 0, 1, kv_01, v_copy)
+            kv_10 = second_matmul(1, 0, h_mx[0])
+            kv_11 = second_matmul(1, 1, h_mx[1], lat_ps, "latent_j")
+            x_bank_0 = turn_x(x_mx_1[1], 0, tp_ps, "tp")
+            x_bank_1 = turn_x(x_mx_1[1], 1, tp_ps, "tp")
+            copy_v(0, 0, 0, kv_00, s_copy)
+            copy_v(0, 0, 1, kv_01, v_copy)
             store_v(0, 0)
-            copy_kv(0, 1, 1, kv_11, s_copy)
+            copy_v(0, 1, 0, kv_10, s_copy)
+            copy_v(0, 1, 1, kv_11, v_copy)
             store_v(0, 1)
-
-            spread_rope(rotated, k_sb[0])
+            copy_nope(0, 0, 0, kv_00, s_copy)
+            copy_nope(0, 0, 1, kv_01, v_copy)
             store_k(0, 0)
+            copy_nope(0, 1, 0, kv_10, s_copy)
+            copy_nope(0, 1, 1, kv_11, v_copy)
             store_k(0, 1)
-            x_bank_1 = turn_x(x_mx_1[0], 1, tp_ps, "tp")
-            copy_x(x_mx_1[0], 0, x_bank, v_copy)
-            copy_x(x_mx_1[0], 1, x_bank_1, s_copy)
             quantise_x(x_mx_1[0], 0)
-            kv = multiply_pair(2, h_mx)
-            x_bank = turn_x(x_mx_1[1], 0, tp_ps, "tp")
-            finish_pair(0, 2, kv, both)
             quantise_x(x_mx_1[0], 1)
-            copy_x(x_mx_1[1], 0, x_bank, v_copy)
-            copy_x(x_mx_1[1], 1, turn_x(x_mx_1[1], 1, tp_ps, "tp"), s_copy)
+            copy_x(x_mx_1[1], 0, x_bank_0, s_copy)
+            copy_x(x_mx_1[1], 1, x_bank_1, v_copy)
             quantise_x(x_mx_1[1], 0)
-            kv = multiply_pair(3, h_mx)
-            latent_1 = new_latent()
             quantise_x(x_mx_1[1], 1)
-            latent_passes(x_mx_1, latent_1, range(0, 2))
+            kv = multiply_pair(2, h_mx)
+            latent_1 = new_latent()
+            latent_passes(x_mx_1, latent_1, range(GROUPS), tiles=(0,))
+            finish_pair(0, 2, kv, (s_copy, s_copy))
+            kv = multiply_pair(3, h_mx)
+            rstd_0 = reciprocal_rms(latent_1, 0)
+            latent_passes(x_mx_1, latent_1, range(GROUPS), tiles=(1,))
             finish_pair(0, 3, kv, both)
             kv = multiply_pair(4, h_mx)
-            latent_passes(x_mx_1, latent_1, range(2, GROUPS))
-            finish_pair(0, 4, kv, both)
+            normed_0, h_0 = new_normed()
+            normalise(normed_0, latent_1, 0, rstd_0, whole)
+            rstd_1 = reciprocal_rms(latent_1, 1)
+            turned_0 = turn_first(normed_0)
+            finish_pair(0, 4, kv, (v_copy, v_copy))
             kv = multiply_pair(5, h_mx)
+            copy_v(0, 5, 0, kv[0], s_copy)
+            copy_nope(0, 5, 0, kv[0], s_copy)
+            h_1 = norm_of_second(latent_1, rstd_1)
+            copy_v(0, 5, 1, kv[1], v_copy)
+            store_v(0, 5)
+            copy_nope(0, 5, 1, kv[1], v_copy)
+            store_k(0, 5)
+            round_h(h_0, turned_0, whole, v_copy)
+            q_0 = quantise_h(h_0)
             r_bank_1 = rope_passes(x_mx_1)
-            finish_pair(0, 5, kv, (v_copy, v_copy))
-
-            def between_second():
-                finish_pair(0, 6, multiply_pair(6, h_mx), (s_copy, s_copy))
-
-            h_mx_1 = norm_head(latent_1, between_second, lambda: None)
+            h_mx_1 = [q_0, quantise_h(h_1)]
             rotated_1 = rotate(r_bank_1)
             spread_rope(rotated_1, k_sb[1])
-            finish_pair(0, 7, multiply_pair(7, h_mx), (s_copy, s_copy))
+            for pair in range(6, N_PAIRS):
+                finish_pair(0, pair, multiply_pair(pair, h_mx), both)
             for pair in range(N_PAIRS):
                 finish_pair(1, pair, multiply_pair(pair, h_mx_1), both)

@@ -29,10 +29,12 @@ THETA = 10000.0
 EPS = 1e-6
 
 GROUPS = D_MODEL // K_PASS
-TOK = SEQ // P
+TOK = BATCH * SEQ // P
+EARLY = 2
 PAIR = 2
 PAIR_COLS = PAIR * HEAD_COLS
-N_PAIRS = HEADS // PAIR
+HALF_HEADS = HEADS // 2
+UNITS = HALF_HEADS // PAIR
 QUADS = 4
 PLANES = 4
 B_PLANE_COLS = B_COLS // PLANES
@@ -53,13 +55,11 @@ def tile_multiheadlatentattention_pb_kernel(
     nc = tc.nc
     with ExitStack() as ctx:
         const = ctx.enter_context(tc.tile_pool(name="const", bufs=1))
-        xin = ctx.enter_context(tc.tile_pool(name="xin", bufs=BATCH))
-        xq = ctx.enter_context(tc.tile_pool(name="xq", bufs=BATCH * TOK))
-        norm = ctx.enter_context(tc.tile_pool(name="norm", bufs=BATCH * TOK))
-        rope = ctx.enter_context(tc.tile_pool(name="rope", bufs=BATCH))
-        outs = ctx.enter_context(tc.tile_pool(name="outs", bufs=BATCH))
+        xq = ctx.enter_context(tc.tile_pool(name="xq", bufs=TOK))
+        norm = ctx.enter_context(tc.tile_pool(name="norm", bufs=TOK))
+        rope = ctx.enter_context(tc.tile_pool(name="rope", bufs=2))
         tp_ps = ctx.enter_context(tc.psum_pool(name="tp_ps", bufs=2))
-        lat_ps = ctx.enter_context(tc.psum_pool(name="lat_ps", bufs=TOK))
+        lat_ps = ctx.enter_context(tc.psum_pool(name="lat_ps", bufs=EARLY))
         rope_ps = ctx.enter_context(tc.psum_pool(name="rope_ps", bufs=1))
         kv_ps = ctx.enter_context(tc.psum_pool(name="kv_ps", bufs=3))
 
@@ -67,8 +67,10 @@ def tile_multiheadlatentattention_pb_kernel(
 
             zeros = const.tile([P, 512], BF16)
             nc.gpsimd.memset(zeros[:].bitcast(F32), 0.0)
-            position = const.tile([P, TOK], I32)
-            nc.gpsimd.iota(position[:], pattern=[[1, TOK]], base=0, channel_multiplier=TOK)
+            partition = const.tile([P, 1], I32)
+            nc.gpsimd.iota(partition[:], pattern=[[1, 1]], base=0, channel_multiplier=1)
+            tile_index = const.tile([P, TOK], I32)
+            nc.gpsimd.iota(tile_index[:], pattern=[[1, TOK]], base=0, channel_multiplier=0)
 
             def keep_warm(moving, count, bank):
                 for i in range(count):
@@ -81,27 +83,23 @@ def tile_multiheadlatentattention_pb_kernel(
             make_identity(nc, ident[:])
             gain_row = const.tile([P, LATENT], BF16)
             nc.gpsimd.memset(gain_row[:].bitcast(F32), 0.0)
-            nc.gpsimd.dma_start(out=gain_row[0:1, :], in_=kv_a_norm_w.rearrange("(o n) -> o n", o=1))
             nc.gpsimd.memset(wb_planes[:].bitcast(F32), 0.0)
 
             wa_words = const.tile([P, GROUPS, A_COLS], U32, align_bytes=64)
             wb_words = const.tile([P, B_COLS], U32, align_bytes=64)
-            x_sb = []
-            for b in range(BATCH):
-                x_b = xin.tile([P, TOK, D_MODEL], BF16, name="x_b")
-                x_sb.append(x_b)
+            x_sb = const.tile([P, TOK, D_MODEL], BF16)
 
-            def load_x(b, j, pieces=1):
+            def load_x(j, pieces=1):
                 width = D_MODEL // pieces
                 for piece in range(pieces):
                     cols = slice(piece * width, (piece + 1) * width)
                     nc.sync.dma_start(
-                        out=x_sb[b][:, j, cols],
-                        in_=x[b].rearrange("(p j) k -> p j k", j=TOK)[:, j, cols],
+                        out=x_sb[:, j, cols],
+                        in_=x.rearrange("b (p j) k -> j p b k", j=TOK)[j][:, :, cols],
                     )
 
-            load_x(0, 0, pieces=2)
-            load_x(0, 1, pieces=2)
+            load_x(0, pieces=2)
+            load_x(1, pieces=2)
             for quad in range(QUADS):
                 nc.sync.dma_start(
                     out=wa_planes[32 * quad : 32 * quad + 16, :].bitcast(I32),
@@ -113,7 +111,8 @@ def tile_multiheadlatentattention_pb_kernel(
                     out=wa_words[:, g, 0:LATENT].bitcast(I32),
                     in_=wa_dram[:, g, 0 : PACK * LATENT].bitcast(I32),
                 )
-            load_x(1, 0)
+            nc.sync.dma_start(out=gain_row[0:1, :], in_=kv_a_norm_w.rearrange("(o n) -> o n", o=1))
+            load_x(2)
             nc.sync.dma_start(
                 out=wa_words[:, :, LATENT:A_COLS].bitcast(I32),
                 in_=wa_dram[:, :, PACK * LATENT : PACK * A_COLS].bitcast(I32),
@@ -125,17 +124,29 @@ def tile_multiheadlatentattention_pb_kernel(
                     .rearrange("r (c n) -> c r n", c=PLANES)
                     .bitcast(I32),
                 )
-            wb_dram = Wkvb_words[0].rearrange("p n t -> p (n t)").bitcast(I32)
-            for c in range(PLANES):
-                cols = slice(c * B_PLANE_COLS, (c + 1) * B_PLANE_COLS)
-                nc.sync.dma_start(out=wb_words[:, cols].bitcast(I32), in_=wb_dram[:, cols])
-                if c == 0:
-                    load_x(1, 1)
+            def load_wb(lo, hi):
+                cols = slice(lo * PAIR_COLS, hi * PAIR_COLS)
+                nc.sync.dma_start(
+                    out=wb_words[:].rearrange("p (e n) -> p e n", e=2)[:, :, cols].bitcast(I32),
+                    in_=Wkvb_words[0].rearrange("p (e n) t -> p e (n t)", e=2)[
+                        :, :, PACK * cols.start : PACK * cols.stop
+                    ].bitcast(I32),
+                )
+
+            load_wb(0, 1)
+            load_x(3)
+            load_wb(1, 2)
+            load_wb(2, UNITS)
 
             powers = const.tile([P, 2, 8], F32)
             nc.vector.memset(powers[:, :, 0:1], 1.0)
             ones = const.tile([P, P], BF16)
             nc.vector.memset(ones[:], 1.0)
+            first_token = const.tile([P, 1], I32)
+            nc.vector.tensor_scalar(
+                out=first_token[:], in0=partition[:], scalar1=1, scalar2=2,
+                op0=ALU.arith_shift_right, op1=ALU.logical_shift_left,
+            )
             for step in range(3):
                 n = 2**step
                 for row in range(2):
@@ -147,8 +158,8 @@ def tile_multiheadlatentattention_pb_kernel(
                     turns = const.tile([P, 2, TOK], F32)
                     for row in range(2):
                         nc.vector.tensor_scalar(
-                            out=turns[:, row, :], in0=position[:],
-                            scalar1=(1 - 2 * row) / (2.0 * math.pi), scalar2=None, op0=ALU.mult,
+                            out=turns[:, row, :], in0=tile_index[:], scalar1=first_token[:, 0:1],
+                            scalar2=(1 - 2 * row) / (2.0 * math.pi), op0=ALU.add, op1=ALU.mult,
                         )
             freq = const.tile([P, HALF], F32)
             nc.vector.tensor_tensor(
@@ -156,46 +167,62 @@ def tile_multiheadlatentattention_pb_kernel(
                 in0=powers[:, 1, :].unsqueeze(2).to_broadcast([P, 8, 8]),
                 in1=powers[:, 0, :].unsqueeze(1).to_broadcast([P, 8, 8]), op=ALU.mult,
             )
+            warm = const.tile([P, 2], F32)
+            nc.scalar.activation(out=warm[:, 0:1], in_=powers[:, 0, 0:1], func=ACT.Sin, scale=0.0)
             freq_pairs = freq[:].rearrange("p (m e) -> p m e", e=2)
             angle = const.tile([P, 2, TOK, HALF], F32)
             for j in range(TOK):
-                nc.vector.tensor_scalar(
-                    out=angle[:, 0, j, :], in0=freq[:],
-                    scalar1=turns[:, 0, j : j + 1], scalar2=0.25, op0=ALU.mult, op1=ALU.add,
-                )
                 carried = angle[:, 1, j, :].rearrange("p (m e) -> p m e", e=2)
-                for e in range(2):
+                if j < EARLY:
                     nc.vector.tensor_scalar(
-                        out=carried[:, :, e], in0=freq_pairs[:, :, 1 - e],
-                        scalar1=turns[:, e, j : j + 1], scalar2=None, op0=ALU.mult,
+                        out=angle[:, 0, j, :], in0=freq[:],
+                        scalar1=turns[:, 0, j : j + 1], scalar2=0.25, op0=ALU.mult, op1=ALU.add,
                     )
+                    for e in range(2):
+                        nc.vector.tensor_scalar(
+                            out=carried[:, :, e], in0=freq_pairs[:, :, 1 - e],
+                            scalar1=turns[:, e, j : j + 1], scalar2=None, op0=ALU.mult,
+                        )
+                else:
+                    nc.scalar.activation(
+                        out=angle[:, 0, j, :], in_=freq[:], func=ACT.Identity,
+                        scale=turns[:, 0, j : j + 1], bias=0.25,
+                    )
+                    for e in range(2):
+                        nc.scalar.activation(
+                            out=carried[:, :, e], in_=freq_pairs[:, :, 1 - e], func=ACT.Identity,
+                            scale=turns[:, e, j : j + 1],
+                        )
             angle_flat = angle[:].rearrange("p c j f -> p (c j f)")
             shifted = const.tile([P, 2 * TOK * HALF], F32)
             nc.vector.tensor_scalar(
                 out=shifted[:], in0=angle_flat, scalar1=ROUND_MAGIC, scalar2=None, op0=ALU.add
             )
             minus_frac = const.tile([P, 2 * TOK * HALF], F32)
-            nc.vector.scalar_tensor_tensor(
-                out=minus_frac[:], in0=shifted[:], scalar=ROUND_MAGIC, in1=angle_flat,
-                op0=ALU.subtract, op1=ALU.subtract,
-            )
             tab = const.tile([P, 2, TOK, HALF], F32)
-            warm = const.tile([P, 2], F32)
-            nc.scalar.activation(out=warm[:, 0:1], in_=powers[:, 0, 0:1], func=ACT.Sin, scale=0.0)
-            nc.scalar.activation(
-                out=tab[:].rearrange("p c j f -> p (c j f)"), in_=minus_frac[:], func=ACT.Sin,
-                scale=-2.0 * math.pi,
-            )
 
-            def new_x(b, j):
+            def subtract_whole_turns():
+                nc.vector.scalar_tensor_tensor(
+                    out=minus_frac[:], in0=shifted[:], scalar=ROUND_MAGIC, in1=angle_flat,
+                    op0=ALU.subtract, op1=ALU.subtract,
+                )
+
+            def take_sines():
+                nc.scalar.activation(
+                    out=tab[:].rearrange("p c j f -> p (c j f)"), in_=minus_frac[:], func=ACT.Sin,
+                    scale=-2.0 * math.pi,
+                )
+
+            def new_x():
                 grouped = xq.tile([P, GROUPS, P, PACK], BF16, align_bytes=64)
                 codes = xq.tile([P, GROUPS * P], U32, align_bytes=64)
                 scales = xq.tile([P, GROUPS * P], U8, align_bytes=64)
-                return b, j, grouped, codes, scales
+                return grouped, codes, scales
 
-            def turn_x(x_mx, half, pool, tag):
-                b, j = x_mx[0], x_mx[1]
-                x_words = x_sb[b][:].bitcast(F32)
+            x_mx = [new_x() for j in range(TOK)]
+
+            def turn_x(j, half, pool, tag):
+                x_words = x_sb[:].bitcast(F32)
                 xt = pool.tile([P, 2, 2, P], F32, tag=tag, name="xt")
                 for gi in range(2):
                     g = 2 * half + gi
@@ -207,14 +234,14 @@ def tile_multiheadlatentattention_pb_kernel(
                         )
                 return xt
 
-            def copy_x(x_mx, half, xt, copy):
+            def copy_x(j, half, xt, copy):
                 copy(
-                    out=x_mx[2][:].bitcast(F32)[:, 2 * half : 2 * half + 2, :, :],
+                    out=x_mx[j][0][:].bitcast(F32)[:, 2 * half : 2 * half + 2, :, :],
                     in_=xt[:].rearrange("p g u k -> p g k u"),
                 )
 
-            def quantise_x(x_mx, half):
-                grouped, codes, scales = x_mx[2], x_mx[3], x_mx[4]
+            def quantise_x(j, half):
+                grouped, codes, scales = x_mx[j]
                 cols = slice(2 * half * P, 2 * (half + 1) * P)
                 nc.vector.quantize_mx(
                     out=codes[:, cols].bitcast(FP8X4),
@@ -222,8 +249,8 @@ def tile_multiheadlatentattention_pb_kernel(
                     in_=grouped[:, 2 * half : 2 * half + 2, :, :].rearrange("p g k t -> p (g k t)"),
                 )
 
-            def first_pass(x_mx, g, n_cols, acc):
-                codes, scales = x_mx[3], x_mx[4]
+            def first_pass(j, g, n_cols, acc):
+                codes, scales = x_mx[j][1], x_mx[j][2]
                 nc.tensor.matmul_mx(
                     out=acc,
                     lhsT=codes[:, g * P : (g + 1) * P].bitcast(FP8X4),
@@ -234,30 +261,20 @@ def tile_multiheadlatentattention_pb_kernel(
                     stop=(g == GROUPS - 1),
                 )
 
-            def new_latent():
-                latent = []
-                for j in range(TOK):
-                    latent_j = lat_ps.tile([P, LATENT], F32, name="latent_j")
-                    latent.append(latent_j)
-                return latent
-
-            def latent_passes(x_mx, latent, groups, tiles=range(TOK)):
+            def latent_passes(j, latent, groups):
                 for g in groups:
-                    for j in tiles:
-                        first_pass(x_mx[j], g, slice(0, LATENT), latent[j][:])
+                    first_pass(j, g, slice(0, LATENT), latent[:])
 
-            def rope_passes(x_mx):
-                bank = rope_ps.tile([P, 512], F32, tag="rope")
-                for j in range(TOK):
+            def rope_passes(bank, tiles):
+                for n, j in enumerate(tiles):
                     for g in range(GROUPS):
-                        first_pass(x_mx[j], g, slice(LATENT, A_COLS), bank[:, j * ROPE : (j + 1) * ROPE])
-                return bank
+                        first_pass(j, g, slice(LATENT, A_COLS), bank[:, n * ROPE : (n + 1) * ROPE])
 
-            def reciprocal_rms(latent, j):
+            def reciprocal_rms(latent):
                 squares = norm.tile([P, LATENT], BF16)
                 mean_sq = norm.tile([P, 1], F32)
                 nc.scalar.activation(
-                    out=squares[:], in_=latent[j][:], func=ACT.Square,
+                    out=squares[:], in_=latent[:], func=ACT.Square,
                     scale=1.0 / math.sqrt(LATENT), accum_out=mean_sq[:],
                 )
                 rstd = norm.tile([P, 1], F32)
@@ -266,10 +283,10 @@ def tile_multiheadlatentattention_pb_kernel(
                 )
                 return rstd
 
-            def normalise(normed, latent, j, rstd, planes):
+            def normalise(normed, latent, rstd, planes):
                 nc.vector.scalar_tensor_tensor(
                     out=normed[:, planes, :],
-                    in0=latent[j][:].rearrange("p (q t) -> p t q", t=PACK)[:, planes, :],
+                    in0=latent[:].rearrange("p (q t) -> p t q", t=PACK)[:, planes, :],
                     scalar=rstd[:, 0:1], in1=gain[:, planes, :], op0=ALU.mult, op1=ALU.mult,
                 )
 
@@ -293,36 +310,41 @@ def tile_multiheadlatentattention_pb_kernel(
                 )
                 return codes, scales
 
-            def rotate(r_bank):
-                prod = rope.tile([P, 2, TOK * ROPE], F32)
+            def rotate(bank, tiles):
+                lo, count = tiles.start, len(tiles)
+                prod = rope.tile([P, 2, EARLY * ROPE], F32)
                 for c in range(2):
                     nc.vector.tensor_tensor(
-                        out=prod[:, c, :].rearrange("p (j r f) -> p j r f", j=TOK, f=HALF),
-                        in0=r_bank[:, 0 : TOK * ROPE].rearrange("p (j r f) -> p j r f", j=TOK, f=HALF),
-                        in1=tab[:, c, :, :].unsqueeze(2).to_broadcast([P, TOK, 2, HALF]), op=ALU.mult,
+                        out=prod[:, c, 0 : count * ROPE].rearrange("p (j r f) -> p j r f", j=count, f=HALF),
+                        in0=bank[:, 0 : count * ROPE].rearrange("p (j r f) -> p j r f", j=count, f=HALF),
+                        in1=tab[:, c, lo : lo + count, :].unsqueeze(2).to_broadcast([P, count, 2, HALF]),
+                        op=ALU.mult,
                     )
-                own = prod[:, 0, :].rearrange("p (m e) -> p m e", e=2)
-                carry = prod[:, 1, :].rearrange("p (m e) -> p m e", e=2)
-                rotated = rope.tile([P, TOK, ROPE], F32)
-                rotated_pairs = rotated[:].rearrange("p j (m e) -> p (j m) e", e=2)
+                own = prod[:, 0, 0 : count * ROPE].rearrange("p (m e) -> p m e", e=2)
+                carry = prod[:, 1, 0 : count * ROPE].rearrange("p (m e) -> p m e", e=2)
+                rotated = rope.tile([P, EARLY * ROPE], F32)
+                rotated_pairs = rotated[:, 0 : count * ROPE].rearrange("p (m e) -> p m e", e=2)
                 for e in range(2):
                     nc.gpsimd.tensor_tensor(
                         out=rotated_pairs[:, :, e], in0=own[:, :, e], in1=carry[:, :, 1 - e], op=ALU.add
                     )
                 return rotated
 
-            def spread_rope(rotated, k_rows):
-                for pair in range(N_PAIRS):
-                    heads = slice(PAIR * pair, PAIR * (pair + 1))
-                    nc.gpsimd.tensor_scalar(
-                        out=k_rows[:, heads, :, NOPE:K_OUT],
-                        in0=rotated[:].unsqueeze(1).to_broadcast([P, PAIR, TOK, ROPE]),
-                        scalar1=1.0, scalar2=0.0, op0=ALU.mult, op1=ALU.add,
-                    )
+            def spread_rope(rotated, tiles, i):
+                lo, count = tiles.start, len(tiles)
+                nc.gpsimd.tensor_scalar(
+                    out=k_sb[:, i, :, lo : lo + count, NOPE:K_OUT],
+                    in0=rotated[:, 0 : count * ROPE].rearrange("p (j f) -> p j f", f=ROPE)
+                    .unsqueeze(1).to_broadcast([P, 2, count, ROPE]),
+                    scalar1=1.0, scalar2=0.0, op0=ALU.mult, op1=ALU.add,
+                )
 
-            def second_matmul(pair, j, h_mx_j, pool=kv_ps, tag="kv"):
-                plane = (pair * PAIR_COLS) // B_PLANE_COLS
-                in_plane = (pair * PAIR_COLS) % B_PLANE_COLS
+            k_sb = const.tile([P, HALF_HEADS, 2, TOK, K_OUT], F32)
+            v_sb = const.tile([P, HALF_HEADS, 2, TOK, VDIM], F32)
+
+            def second_matmul(m, e, h_mx_j, pool=kv_ps, tag="kv"):
+                col = (m + UNITS * e) * PAIR_COLS
+                plane, in_plane = col // B_PLANE_COLS, col % B_PLANE_COLS
                 codes, scales = h_mx_j
                 kv = pool.tile([P, 512], F32, tag=tag, name="kv")
                 for lo, hi in ((0, 256), (256, PAIR_COLS)):
@@ -330,91 +352,56 @@ def tile_multiheadlatentattention_pb_kernel(
                         out=kv[:, lo:hi],
                         lhsT=codes[:].bitcast(FP8X4),
                         lhsT_scale=scales[:],
-                        rhs=wb_words[:, pair * PAIR_COLS + lo : pair * PAIR_COLS + hi].bitcast(FP8X4),
+                        rhs=wb_words[:, col + lo : col + hi].bitcast(FP8X4),
                         rhs_scale=wb_planes[4 * plane : P, in_plane + lo : in_plane + hi],
                         start=True,
                         stop=True,
                     )
                 return kv
 
-            def heads_of(pair):
-                return slice(PAIR * pair, PAIR * (pair + 1))
-
             def by_head(kv):
                 return kv[:, 0:PAIR_COLS].rearrange("p (h c) -> p h c", h=PAIR)
 
-            def copy_v(b, pair, j, kv, copy):
-                copy(out=v_sb[b][:, heads_of(pair), j, :], in_=by_head(kv)[:, :, NOPE:HEAD_COLS])
-
-            def copy_nope(b, pair, j, kv, copy):
-                copy(out=k_sb[b][:, heads_of(pair), j, 0:NOPE], in_=by_head(kv)[:, :, 0:NOPE])
-
-            def store_v(b, pair):
-                heads = heads_of(pair)
-                nc.sync.dma_start(
-                    out=out_1[b, heads].rearrange("h (p j) d -> p h (j d)", j=TOK),
-                    in_=v_sb[b][:, heads, :, :].rearrange("p h j d -> p h (j d)"),
+            def copy_v(m, e, j, kv, copy):
+                copy(
+                    out=v_sb[:, PAIR * m : PAIR * (m + 1), e, j, :],
+                    in_=by_head(kv)[:, :, NOPE:HEAD_COLS],
                 )
 
-            def store_k(b, pair):
-                heads = heads_of(pair)
-                nc.sync.dma_start(
-                    out=out_0[b, heads].rearrange("h (p j) d -> p h (j d)", j=TOK),
-                    in_=k_sb[b][:, heads, :, :].rearrange("p h j d -> p h (j d)"),
+            def copy_nope(m, e, j, kv, copy):
+                copy(
+                    out=k_sb[:, PAIR * m : PAIR * (m + 1), e, j, 0:NOPE],
+                    in_=by_head(kv)[:, :, 0:NOPE],
                 )
 
-            def multiply_pair(pair, h_mx):
-                return [second_matmul(pair, j, h_mx[j]) for j in range(TOK)]
+            def store_bank(out, rows, width, m, e, tiles):
+                lo, hi = tiles.start * width, tiles.stop * width
+                by_head = out.rearrange("b h (p j) d -> h p b (j d)", j=TOK)
+                for i in range(PAIR * m, PAIR * (m + 1)):
+                    nc.sync.dma_start(
+                        out=by_head[i + HALF_HEADS * e][:, :, lo:hi],
+                        in_=rows[:, i, e, :, :].rearrange("p j d -> p (j d)")[:, lo:hi],
+                    )
 
-            def finish_pair(b, pair, kv, copies):
-                for j in range(TOK):
-                    copy_v(b, pair, j, kv[j], copies[j])
-                store_v(b, pair)
-                for j in range(TOK):
-                    copy_nope(b, pair, j, kv[j], copies[j])
-                store_k(b, pair)
-
-            k_sb = []
-            v_sb = []
-            for b in range(BATCH):
-                k_b = outs.tile([P, HEADS, TOK, K_OUT], F32, name="k_b")
-                v_b = outs.tile([P, HEADS, TOK, VDIM], F32, name="v_b")
-                k_sb.append(k_b)
-                v_sb.append(v_b)
+            def store_unit(out, rows, width, m, tiles):
+                lo, hi = tiles.start * width, tiles.stop * width
+                by_i = out.rearrange("b (e i) (p j) d -> i p (b e) (j d)", e=2, j=TOK)
+                for i in range(PAIR * m, PAIR * (m + 1)):
+                    nc.sync.dma_start(
+                        out=by_i[i][:, :, lo:hi],
+                        in_=rows[:, i, :, :, :].rearrange("p e j d -> p e (j d)")[:, :, lo:hi],
+                    )
 
             v_copy, s_copy = nc.vector.tensor_copy, nc.scalar.copy
             both = (v_copy, s_copy)
-            x_mx = [new_x(0, 0), new_x(0, 1)]
-            warm_bank = rope_ps.tile([P, 512], F32, tag="rope")
-            keep_warm(zeros[:], WARM_START, warm_bank[:])
-            xt = [turn_x(x_mx[0], 0, tp_ps, "tp"), turn_x(x_mx[0], 1, tp_ps, "tp")]
-            gain_bank = kv_ps.tile([P, 512], F32, tag="kv")
-            copy_x(x_mx[0], 0, xt[0], v_copy)
-            copy_x(x_mx[0], 1, xt[1], s_copy)
-            keep_warm(zeros[:], WARM_TURN, warm_bank[:])
-            xt = [turn_x(x_mx[1], 0, kv_ps, "kv"), turn_x(x_mx[1], 1, kv_ps, "kv")]
-            keep_warm(zeros[:], WARM_TURN, warm_bank[:])
-            quantise_x(x_mx[0], 0)
-            copy_x(x_mx[1], 0, xt[0], s_copy)
-            quantise_x(x_mx[0], 1)
-            copy_x(x_mx[1], 1, xt[1], v_copy)
-            latent = new_latent()
-            latent_passes(x_mx, latent, range(0, 1), tiles=(0,))
-            nc.tensor.matmul(out=gain_bank[:], lhsT=ones[:], rhs=gain_row[:], start=True, stop=True)
-            gain = const.tile([P, PACK, P], F32)
-            latent_passes(x_mx, latent, range(1, 2), tiles=(0,))
-            quantise_x(x_mx[1], 0)
-            nc.scalar.activation(
-                out=warm[:, 1:2], in_=tab[:, 0, 0, 0:1], func=ACT.Abs_reciprocal_sqrt, bias=1.0, scale=0.0
-            )
-            quantise_x(x_mx[1], 1)
-            v_copy(out=gain[:], in_=gain_bank[:].rearrange("p (q t) -> p t q", t=PACK))
-            latent_passes(x_mx, latent, range(0, 2), tiles=(1,))
-            for j in range(TOK):
-                latent_passes(x_mx, latent, range(2, GROUPS), tiles=(j,))
-            x_mx_1 = [new_x(1, 0), new_x(1, 1)]
-            x_bank_0 = turn_x(x_mx_1[0], 0, kv_ps, "kv")
-            r_bank = rope_passes(x_mx)
+            early, late, every = range(0, EARLY), range(EARLY, TOK), range(0, TOK)
+
+            def new_latent():
+                latent = []
+                for j in range(2):
+                    latent_j = lat_ps.tile([P, LATENT], F32, name="latent_j")
+                    latent.append(latent_j)
+                return latent
 
             whole, halves = slice(0, PACK), (slice(0, PACK // 2), slice(PACK // 2, PACK))
 
@@ -428,84 +415,161 @@ def tile_multiheadlatentattention_pb_kernel(
                 turn_h(turned, normed, whole)
                 return turned
 
-            def norm_of_second(latent, rstd):
+            def norm_of_second(latent_j, rstd):
                 normed, h_grouped = new_normed()
                 for half, pool, tag in zip(halves, (tp_ps, kv_ps), ("tp", "kv")):
-                    normalise(normed, latent, 1, rstd, half)
+                    normalise(normed, latent_j, rstd, half)
                     turned = pool.tile([P, PACK, P], F32, tag=tag)
                     turn_h(turned, normed, half)
                     round_h(h_grouped, turned, half, s_copy)
                 return h_grouped
 
-            rstd_0 = reciprocal_rms(latent, 0)
-            normed_0, h_0 = new_normed()
-            normalise(normed_0, latent, 0, rstd_0, whole)
-            rstd_1 = reciprocal_rms(latent, 1)
-            copy_x(x_mx_1[0], 0, x_bank_0, s_copy)
+            warm_bank = rope_ps.tile([P, 512], F32, tag="rope")
+            keep_warm(zeros[:], WARM_START, warm_bank[:])
+            xt = [turn_x(0, half, tp_ps, "tp") for half in range(2)]
+            copy_x(0, 0, xt[0], v_copy)
+            copy_x(0, 1, xt[1], s_copy)
+            keep_warm(zeros[:], WARM_TURN, warm_bank[:])
+            xt = [turn_x(1, half, kv_ps, "kv") for half in range(2)]
+            keep_warm(zeros[:], WARM_TURN, warm_bank[:])
+            quantise_x(0, 0)
+            subtract_whole_turns()
+            copy_x(1, 0, xt[0], s_copy)
+            take_sines()
+            quantise_x(0, 1)
+            quantise_x(1, 0)
+            copy_x(1, 1, xt[1], v_copy)
+            nc.scalar.activation(
+                out=warm[:, 1:2], in_=tab[:, 0, 0, 0:1], func=ACT.Abs_reciprocal_sqrt, bias=1.0, scale=0.0
+            )
+            quantise_x(1, 1)
+            latent = new_latent()
+            for j in early:
+                latent_passes(j, latent[j], range(0, 2))
+            latent_passes(0, latent[0], range(2, GROUPS))
+            gain = const.tile([P, PACK, P], F32)
+            gain_bank = kv_ps.tile([P, 512], F32, tag="kv")
+            nc.tensor.matmul(out=gain_bank[:], lhsT=ones[:], rhs=gain_row[:], start=True, stop=True)
+            v_copy(out=gain[:], in_=gain_bank[:].rearrange("p (q t) -> p t q", t=PACK))
+            latent_passes(1, latent[1], range(2, GROUPS))
+            x_bank_0 = turn_x(2, 0, kv_ps, "kv")
             warm_bank = kv_ps.tile([P, 512], F32, tag="kv")
             keep_warm(zeros[:], WARM_NORM, warm_bank[:])
-            turned_0 = turn_first(normed_0)
-            h_1 = norm_of_second(latent, rstd_1)
-            x_bank_1 = turn_x(x_mx_1[0], 1, kv_ps, "kv")
-            round_h(h_0, turned_0, whole, v_copy)
-            copy_x(x_mx_1[0], 1, x_bank_1, s_copy)
-            h_mx = [quantise_h(h_0), quantise_h(h_1)]
-            rotated = rotate(r_bank)
-            spread_rope(rotated, k_sb[0])
-
-            kv_00 = second_matmul(0, 0, h_mx[0])
-            kv_01 = second_matmul(0, 1, h_mx[1])
-            kv_10 = second_matmul(1, 0, h_mx[0])
-            kv_11 = second_matmul(1, 1, h_mx[1], lat_ps, "latent_j")
-            x_bank_0 = turn_x(x_mx_1[1], 0, tp_ps, "tp")
-            x_bank_1 = turn_x(x_mx_1[1], 1, tp_ps, "tp")
-            copy_v(0, 0, 0, kv_00, s_copy)
-            copy_v(0, 0, 1, kv_01, v_copy)
-            store_v(0, 0)
-            copy_v(0, 1, 0, kv_10, s_copy)
-            copy_v(0, 1, 1, kv_11, v_copy)
-            store_v(0, 1)
-            copy_nope(0, 0, 0, kv_00, s_copy)
-            copy_nope(0, 0, 1, kv_01, v_copy)
-            store_k(0, 0)
-            copy_nope(0, 1, 0, kv_10, s_copy)
-            copy_nope(0, 1, 1, kv_11, v_copy)
-            store_k(0, 1)
-            quantise_x(x_mx_1[0], 0)
-            quantise_x(x_mx_1[0], 1)
-            copy_x(x_mx_1[1], 0, x_bank_0, s_copy)
-            copy_x(x_mx_1[1], 1, x_bank_1, v_copy)
-            quantise_x(x_mx_1[1], 0)
-            quantise_x(x_mx_1[1], 1)
-            kv = multiply_pair(2, h_mx)
-            latent_1 = new_latent()
-            latent_passes(x_mx_1, latent_1, range(GROUPS), tiles=(0,))
-            finish_pair(0, 2, kv, (s_copy, s_copy))
-            kv = multiply_pair(3, h_mx)
-            rstd_0 = reciprocal_rms(latent_1, 0)
-            latent_passes(x_mx_1, latent_1, range(GROUPS), tiles=(1,))
-            finish_pair(0, 3, kv, both)
-            kv = multiply_pair(4, h_mx)
+            rstd_0 = reciprocal_rms(latent[0])
             normed_0, h_0 = new_normed()
-            normalise(normed_0, latent_1, 0, rstd_0, whole)
-            rstd_1 = reciprocal_rms(latent_1, 1)
+            normalise(normed_0, latent[0], rstd_0, whole)
+            rstd_1 = reciprocal_rms(latent[1])
+            copy_x(2, 0, x_bank_0, s_copy)
             turned_0 = turn_first(normed_0)
-            finish_pair(0, 4, kv, (v_copy, v_copy))
-            kv = multiply_pair(5, h_mx)
-            copy_v(0, 5, 0, kv[0], s_copy)
-            copy_nope(0, 5, 0, kv[0], s_copy)
-            h_1 = norm_of_second(latent_1, rstd_1)
-            copy_v(0, 5, 1, kv[1], v_copy)
-            store_v(0, 5)
-            copy_nope(0, 5, 1, kv[1], v_copy)
-            store_k(0, 5)
+            h_1 = norm_of_second(latent[1], rstd_1)
+            r_bank = rope_ps.tile([P, 512], F32, tag="rope")
+            rope_passes(r_bank, early)
+            round_h(h_0, turned_0, whole, v_copy)
+            h_mx = [quantise_h(h_0), quantise_h(h_1)]
+            rotated = rotate(r_bank, early)
+            for i in range(HALF_HEADS):
+                spread_rope(rotated, early, i)
+
+            def multiply(m, e, tiles):
+                return [second_matmul(m, e, h_mx[j]) for j in tiles]
+
+            def copy_vs(m, e, tiles, kv, copies):
+                for j, kv_j, copy in zip(tiles, kv, copies):
+                    copy_v(m, e, j, kv_j, copy)
+
+            def copy_nopes(m, e, tiles, kv, copies):
+                for j, kv_j, copy in zip(tiles, kv, copies):
+                    copy_nope(m, e, j, kv_j, copy)
+
+            def store_v_of_bank(m, e, tiles):
+                store_bank(out_1, v_sb, VDIM, m, e, tiles)
+
+            def store_k_of_bank(m, e, tiles):
+                store_bank(out_0, k_sb, K_OUT, m, e, tiles)
+
+            def store_v_of_unit(m, tiles):
+                store_unit(out_1, v_sb, VDIM, m, tiles)
+
+            def store_k_of_unit(m, tiles):
+                store_unit(out_0, k_sb, K_OUT, m, tiles)
+
+            def finish_early(m, e, kv, copies):
+                copy_vs(m, e, early, kv, copies)
+                store_v_of_bank(m, e, early)
+                copy_nopes(m, e, early, kv, copies)
+                store_k_of_bank(m, e, early)
+
+            kv_0 = multiply(0, 0, early)
+            kv_1 = [second_matmul(0, 1, h_mx[0]), second_matmul(0, 1, h_mx[1], lat_ps, "latent_j")]
+            x_bank_1 = turn_x(2, 1, tp_ps, "tp")
+            x_bank_2 = turn_x(3, 0, tp_ps, "tp")
+            swapped = (s_copy, v_copy)
+            copy_vs(0, 0, early, kv_0, swapped)
+            store_v_of_bank(0, 0, early)
+            copy_vs(0, 1, early, kv_1, swapped)
+            store_v_of_bank(0, 1, early)
+            copy_nopes(0, 0, early, kv_0, swapped)
+            store_k_of_bank(0, 0, early)
+            copy_nopes(0, 1, early, kv_1, swapped)
+            store_k_of_bank(0, 1, early)
+            kv = multiply(1, 0, early)
+            quantise_x(2, 0)
+            copy_x(2, 1, x_bank_1, s_copy)
+            copy_x(3, 0, x_bank_2, v_copy)
+            quantise_x(2, 1)
+            x_bank_3 = turn_x(3, 1, tp_ps, "tp")
+            quantise_x(3, 0)
+            copy_x(3, 1, x_bank_3, v_copy)
+            quantise_x(3, 1)
+            latent = new_latent()
+            latent_passes(2, latent[0], range(GROUPS))
+            finish_early(1, 0, kv, (s_copy, s_copy))
+            kv = multiply(1, 1, early)
+            rstd_0 = reciprocal_rms(latent[0])
+            latent_passes(3, latent[1], range(GROUPS))
+            finish_early(1, 1, kv, both)
+            kv = multiply(2, 0, early)
+            normed_0, h_0 = new_normed()
+            normalise(normed_0, latent[0], rstd_0, whole)
+            rstd_1 = reciprocal_rms(latent[1])
+            turned_0 = turn_first(normed_0)
+            copy_nopes(2, 0, early, kv, (v_copy, v_copy))
+            store_k_of_bank(2, 0, early)
+            copy_vs(2, 0, early, kv, (v_copy, v_copy))
+            kv = multiply(2, 1, early)
+            copy_nope(2, 1, 0, kv[0], s_copy)
+            copy_v(2, 1, 0, kv[0], s_copy)
+            h_1 = norm_of_second(latent[1], rstd_1)
+            copy_nope(2, 1, 1, kv[1], v_copy)
+            store_k_of_bank(2, 1, early)
+            copy_v(2, 1, 1, kv[1], v_copy)
             round_h(h_0, turned_0, whole, v_copy)
             q_0 = quantise_h(h_0)
-            r_bank_1 = rope_passes(x_mx_1)
-            h_mx_1 = [q_0, quantise_h(h_1)]
-            rotated_1 = rotate(r_bank_1)
-            spread_rope(rotated_1, k_sb[1])
-            for pair in range(6, N_PAIRS):
-                finish_pair(0, pair, multiply_pair(pair, h_mx), both)
-            for pair in range(N_PAIRS):
-                finish_pair(1, pair, multiply_pair(pair, h_mx_1), both)
+            r_bank = rope_ps.tile([P, 512], F32, tag="rope")
+            rope_passes(r_bank, late)
+            h_mx += [q_0, quantise_h(h_1)]
+            rotated = rotate(r_bank, late)
+            for i in range(HALF_HEADS):
+                spread_rope(rotated, late, (i + PAIR * 2) % HALF_HEADS)
+
+            def finish(m, e, tiles):
+                kv = multiply(m, e, tiles)
+                copy_vs(m, e, tiles, kv, both)
+                copy_nopes(m, e, tiles, kv, both)
+
+            for e in range(2):
+                kv = multiply(2, e, late)
+                copy_vs(2, e, late, kv, both)
+                store_v_of_bank(2, e, every)
+                copy_nopes(2, e, late, kv, both)
+                store_k_of_bank(2, e, late)
+            for tiles in (early, late):
+                for e in range(2):
+                    finish(3, e, tiles)
+            store_v_of_unit(3, every)
+            store_k_of_unit(3, every)
+            for m in range(2):
+                for e in range(2):
+                    finish(m, e, late)
+                store_v_of_unit(m, late)
+                store_k_of_unit(m, late)

@@ -533,43 +533,39 @@ def tile_multiheadlatentattention_pb_kernel(
             normalise(normed_0, latent[0], rstd_0, whole)
             rstd_1 = reciprocal_rms(latent[1])
             turned_0 = turn_first(normed_0)
-            copy_nopes(2, 0, early, kv, (v_copy, v_copy))
-            store_k_of_bank(2, 0, early)
-            copy_vs(2, 0, early, kv, (v_copy, v_copy))
+            finish_early(2, 0, kv, (v_copy, v_copy))
             kv = multiply(2, 1, early)
-            copy_nope(2, 1, 0, kv[0], s_copy)
             copy_v(2, 1, 0, kv[0], s_copy)
+            copy_nope(2, 1, 0, kv[0], s_copy)
             h_1 = norm_of_second(latent[1], rstd_1)
+            copy_v(2, 1, 1, kv[1], v_copy)
+            store_v_of_bank(2, 1, early)
             copy_nope(2, 1, 1, kv[1], v_copy)
             store_k_of_bank(2, 1, early)
-            copy_v(2, 1, 1, kv[1], v_copy)
             round_h(h_0, turned_0, whole, v_copy)
             q_0 = quantise_h(h_0)
             r_bank = rope_ps.tile([P, 512], F32, tag="rope")
             rope_passes(r_bank, late)
             h_mx += [q_0, quantise_h(h_1)]
-            rotated = rotate(r_bank, late)
-            for i in range(HALF_HEADS):
-                spread_rope(rotated, late, (i + PAIR * 2) % HALF_HEADS)
 
             def finish(m, e, tiles):
                 kv = multiply(m, e, tiles)
                 copy_vs(m, e, tiles, kv, both)
                 copy_nopes(m, e, tiles, kv, both)
 
-            for e in range(2):
-                kv = multiply(2, e, late)
-                copy_vs(2, e, late, kv, both)
-                store_v_of_bank(2, e, every)
-                copy_nopes(2, e, late, kv, both)
-                store_k_of_bank(2, e, late)
+            rotated = rotate(r_bank, late)
+            for i in range(HALF_HEADS):
+                spread_rope(rotated, late, i)
+            for m in range(UNITS - 1):
+                for e in range(2):
+                    copies = (s_copy, s_copy) if (m, e) == (0, 0) else both
+                    kv = multiply(m, e, late)
+                    copy_vs(m, e, late, kv, copies)
+                    store_v_of_bank(m, e, late)
+                    copy_nopes(m, e, late, kv, copies)
+                store_k_of_unit(m, late)
             for tiles in (early, late):
                 for e in range(2):
-                    finish(3, e, tiles)
-            store_v_of_unit(3, every)
-            store_k_of_unit(3, every)
-            for m in range(2):
-                for e in range(2):
-                    finish(m, e, late)
-                store_v_of_unit(m, late)
-                store_k_of_unit(m, late)
+                    finish(UNITS - 1, e, tiles)
+            store_v_of_unit(UNITS - 1, every)
+            store_k_of_unit(UNITS - 1, every)

@@ -40,9 +40,9 @@ PLANES = 4
 B_PLANE_COLS = B_COLS // PLANES
 
 
-WARM_START = 4
-WARM_TURN = 1
-WARM_NORM = 1
+WARM_START = 5
+WARM_TURN = (2, 1)
+WARM_NORM = 2
 
 ROUND_MAGIC = 1.5 * 2.0**23
 
@@ -429,9 +429,9 @@ def tile_multiheadlatentattention_pb_kernel(
             xt = [turn_x(0, half, tp_ps, "tp") for half in range(2)]
             copy_x(0, 0, xt[0], v_copy)
             copy_x(0, 1, xt[1], s_copy)
-            keep_warm(zeros[:], WARM_TURN, warm_bank[:])
+            keep_warm(zeros[:], WARM_TURN[0], warm_bank[:])
             xt = [turn_x(1, half, kv_ps, "kv") for half in range(2)]
-            keep_warm(zeros[:], WARM_TURN, warm_bank[:])
+            keep_warm(zeros[:], WARM_TURN[1], warm_bank[:])
             quantise_x(0, 0)
             subtract_whole_turns()
             copy_x(1, 0, xt[0], s_copy)

import math
from contextlib import ExitStack

import concourse.mybir as mybir
from concourse.masks import make_identity

F32 = mybir.dt.float32
BF16 = mybir.dt.bfloat16
I32 = mybir.dt.int32
U32 = mybir.dt.uint32
U8 = mybir.dt.uint8
FP8X4 = mybir.dt.float8_e4m3fn_x4
ALU = mybir.AluOpType
ACT = mybir.ActivationFunctionType

P = 128
PACK = 4
K_PASS = P * PACK

BATCH, SEQ, D_MODEL = 2, 256, 2048
LATENT, ROPE = 512, 128
HALF = ROPE // 2
HEADS, NOPE, VDIM = 16, 64, 128
A_COLS = LATENT + ROPE
HEAD_COLS = NOPE + VDIM
B_COLS = HEADS * HEAD_COLS
K_OUT = NOPE + ROPE
THETA = 10000.0
EPS = 1e-6

GROUPS = D_MODEL // K_PASS
TOK = BATCH * SEQ // P
EARLY = 2
PAIR = 2
PAIR_COLS = PAIR * HEAD_COLS
HALF_HEADS = HEADS // 2
UNITS = HALF_HEADS // PAIR
QUADS = 4
PLANES = 4
B_PLANE_COLS = B_COLS // PLANES


WARM_START = 5
WARM_TURN = (2, 1)
WARM_NORM = 2

ROUND_MAGIC = 1.5 * 2.0**23

FLOPS = 2 * BATCH * SEQ * (D_MODEL * A_COLS + LATENT * B_COLS)


def tile_multiheadlatentattention_pb_kernel(
    tc, x, Wkva_words, Wkva_scales, kv_a_norm_w, Wkvb_words, Wkvb_scales, out_0, out_1
):
    nc = tc.nc
    with ExitStack() as ctx:
        const = ctx.enter_context(tc.tile_pool(name="const", bufs=1))
        xq = ctx.enter_context(tc.tile_pool(name="xq", bufs=TOK))
        norm = ctx.enter_context(tc.tile_pool(name="norm", bufs=TOK))
        rope = ctx.enter_context(tc.tile_pool(name="rope", bufs=2))
        tp_ps = ctx.enter_context(tc.psum_pool(name="tp_ps", bufs=2))
        lat_ps = ctx.enter_context(tc.psum_pool(name="lat_ps", bufs=EARLY))
        rope_ps = ctx.enter_context(tc.psum_pool(name="rope_ps", bufs=1))
        kv_ps = ctx.enter_context(tc.psum_pool(name="kv_ps", bufs=3))

        with tc.manual_schedule():

            zeros = const.tile([P, 512], BF16)
            nc.gpsimd.memset(zeros[:].bitcast(F32), 0.0)
            partition = const.tile([P, 1], I32)
            nc.gpsimd.iota(partition[:], pattern=[[1, 1]], base=0, channel_multiplier=1)
            tile_index = const.tile([P, TOK], I32)
            nc.gpsimd.iota(tile_index[:], pattern=[[1, TOK]], base=0, channel_multiplier=0)

            def keep_warm(moving, count, bank):
                for i in range(count):
                    nc.tensor.matmul(out=bank, lhsT=zeros[:, 0:P], rhs=moving, start=True, stop=True)

            wa_planes = const.tile([P, A_COLS], U8, align_bytes=64)
            wb_planes = const.tile([P, B_PLANE_COLS], U8, align_bytes=64)
            nc.gpsimd.memset(wa_planes[:].bitcast(F32), 0.0)
            ident = const.tile([P, P], F32)
            make_identity(nc, ident[:])
            gain_row = const.tile([P, LATENT], BF16)
            nc.gpsimd.memset(gain_row[:].bitcast(F32), 0.0)
            nc.gpsimd.memset(wb_planes[:].bitcast(F32), 0.0)

            wa_words = const.tile([P, GROUPS, A_COLS], U32, align_bytes=64)
            wb_words = const.tile([P, B_COLS], U32, align_bytes=64)
            x_sb = const.tile([P, TOK, D_MODEL], BF16)

            def load_x(j, pieces=1):
                width = D_MODEL // pieces
                for piece in range(pieces):
                    cols = slice(piece * width, (piece + 1) * width)
                    nc.sync.dma_start(
                        out=x_sb[:, j, cols],
                        in_=x.rearrange("b (p j) k -> j p b k", j=TOK)[j][:, :, cols],
                    )

            load_x(0, pieces=2)
            load_x(1, pieces=2)
            for quad in range(QUADS):
                nc.sync.dma_start(
                    out=wa_planes[32 * quad : 32 * quad + 16, :].bitcast(I32),
                    in_=Wkva_scales[:, 4 * quad : 4 * quad + 4, :].bitcast(I32),
                )
            wa_dram = Wkva_words.rearrange("g p n t -> p g (n t)")
            for g in range(GROUPS):
                nc.sync.dma_start(
                    out=wa_words[:, g, 0:LATENT].bitcast(I32),
                    in_=wa_dram[:, g, 0 : PACK * LATENT].bitcast(I32),
                )
            nc.sync.dma_start(out=gain_row[0:1, :], in_=kv_a_norm_w.rearrange("(o n) -> o n", o=1))
            load_x(2)
            nc.sync.dma_start(
                out=wa_words[:, :, LATENT:A_COLS].bitcast(I32),
                in_=wa_dram[:, :, PACK * LATENT : PACK * A_COLS].bitcast(I32),
            )
            for quad in range(QUADS):
                nc.sync.dma_start(
                    out=wb_planes[32 * quad : 32 * quad + 16, :].bitcast(I32),
                    in_=Wkvb_scales[0, 4 * quad : 4 * quad + 4, :]
                    .rearrange("r (c n) -> c r n", c=PLANES)
                    .bitcast(I32),
                )
            def load_wb(lo, hi):
                cols = slice(lo * PAIR_COLS, hi * PAIR_COLS)
                nc.sync.dma_start(
                    out=wb_words[:].rearrange("p (e n) -> p e n", e=2)[:, :, cols].bitcast(I32),
                    in_=Wkvb_words[0].rearrange("p (e n) t -> p e (n t)", e=2)[
                        :, :, PACK * cols.start : PACK * cols.stop
                    ].bitcast(I32),
                )

            load_wb(0, 1)
            load_x(3)
            load_wb(1, 2)
            load_wb(2, UNITS)

            powers = const.tile([P, 2, 8], F32)
            nc.vector.memset(powers[:, :, 0:1], 1.0)
            ones = const.tile([P, P], BF16)
            nc.vector.memset(ones[:], 1.0)
            first_token = const.tile([P, 1], I32)
            nc.vector.tensor_scalar(
                out=first_token[:], in0=partition[:], scalar1=1, scalar2=2,
                op0=ALU.arith_shift_right, op1=ALU.logical_shift_left,
            )
            for step in range(3):
                n = 2**step
                for row in range(2):
                    nc.vector.tensor_scalar(
                        out=powers[:, row, n : 2 * n], in0=powers[:, row, 0:n],
                        scalar1=math.pow(THETA, -n * 8**row / 64.0), scalar2=None, op0=ALU.mult,
                    )
                if step == 0:
                    turns = const.tile([P, 2, TOK], F32)
                    for row in range(2):
                        nc.vector.tensor_scalar(
                            out=turns[:, row, :], in0=tile_index[:], scalar1=first_token[:, 0:1],
                            scalar2=(1 - 2 * row) / (2.0 * math.pi), op0=ALU.add, op1=ALU.mult,
                        )
            freq = const.tile([P, HALF], F32)
            nc.vector.tensor_tensor(
                out=freq[:].rearrange("p (a i) -> p a i", i=8),
                in0=powers[:, 1, :].unsqueeze(2).to_broadcast([P, 8, 8]),
                in1=powers[:, 0, :].unsqueeze(1).to_broadcast([P, 8, 8]), op=ALU.mult,
            )
            warm = const.tile([P, 2], F32)
            nc.scalar.activation(out=warm[:, 0:1], in_=powers[:, 0, 0:1], func=ACT.Sin, scale=0.0)
            freq_pairs = freq[:].rearrange("p (m e) -> p m e", e=2)
            angle = const.tile([P, 2, TOK, HALF], F32)
            for j in range(TOK):
                carried = angle[:, 1, j, :].rearrange("p (m e) -> p m e", e=2)
                if j < EARLY:
                    nc.vector.tensor_scalar(
                        out=angle[:, 0, j, :], in0=freq[:],
                        scalar1=turns[:, 0, j : j + 1], scalar2=0.25, op0=ALU.mult, op1=ALU.add,
                    )
                    for e in range(2):
                        nc.vector.tensor_scalar(
                            out=carried[:, :, e], in0=freq_pairs[:, :, 1 - e],
                            scalar1=turns[:, e, j : j + 1], scalar2=None, op0=ALU.mult,
                        )
                else:
                    nc.scalar.activation(
                        out=angle[:, 0, j, :], in_=freq[:], func=ACT.Identity,
                        scale=turns[:, 0, j : j + 1], bias=0.25,
                    )
                    for e in range(2):
                        nc.scalar.activation(
                            out=carried[:, :, e], in_=freq_pairs[:, :, 1 - e], func=ACT.Identity,
                            scale=turns[:, e, j : j + 1],
                        )
            angle_flat = angle[:].rearrange("p c j f -> p (c j f)")
            shifted = const.tile([P, 2 * TOK * HALF], F32)
            nc.vector.tensor_scalar(
                out=shifted[:], in0=angle_flat, scalar1=ROUND_MAGIC, scalar2=None, op0=ALU.add
            )
            minus_frac = const.tile([P, 2 * TOK * HALF], F32)
            tab = const.tile([P, 2, TOK, HALF], F32)

            def subtract_whole_turns():
                nc.vector.scalar_tensor_tensor(
                    out=minus_frac[:], in0=shifted[:], scalar=ROUND_MAGIC, in1=angle_flat,
                    op0=ALU.subtract, op1=ALU.subtract,
                )

            def take_sines():
                nc.scalar.activation(
                    out=tab[:].rearrange("p c j f -> p (c j f)"), in_=minus_frac[:], func=ACT.Sin,
                    scale=-2.0 * math.pi,
                )

            def new_x():
                grouped = xq.tile([P, GROUPS, P, PACK], BF16, align_bytes=64)
                codes = xq.tile([P, GROUPS * P], U32, align_bytes=64)
                scales = xq.tile([P, GROUPS * P], U8, align_bytes=64)
                return grouped, codes, scales

            x_mx = [new_x() for j in range(TOK)]

            def turn_x(j, half, pool, tag):
                x_words = x_sb[:].bitcast(F32)
                xt = pool.tile([P, 2, 2, P], F32, tag=tag, name="xt")
                for gi in range(2):
                    g = 2 * half + gi
                    for u in range(2):
                        nc.tensor.transpose(
                            out=xt[:, gi, u, :],
                            in_=x_words[:, j, 256 * g + u : 256 * (g + 1) : 2],
                            identity=ident[:],
                        )
                return xt

            def copy_x(j, half, xt, copy):
                copy(
                    out=x_mx[j][0][:].bitcast(F32)[:, 2 * half : 2 * half + 2, :, :],
                    in_=xt[:].rearrange("p g u k -> p g k u"),
                )

            def quantise_x(j, half):
                grouped, codes, scales = x_mx[j]
                cols = slice(2 * half * P, 2 * (half + 1) * P)
                nc.vector.quantize_mx(
                    out=codes[:, cols].bitcast(FP8X4),
                    scales=scales[:, cols],
                    in_=grouped[:, 2 * half : 2 * half + 2, :, :].rearrange("p g k t -> p (g k t)"),
                )

            def first_pass(j, g, n_cols, acc):
                codes, scales = x_mx[j][1], x_mx[j][2]
                nc.tensor.matmul_mx(
                    out=acc,
                    lhsT=codes[:, g * P : (g + 1) * P].bitcast(FP8X4),
                    lhsT_scale=scales[:, g * P : (g + 1) * P],
                    rhs=wa_words[:, g, n_cols].bitcast(FP8X4),
                    rhs_scale=wa_planes[4 * g : P, n_cols],
                    start=(g == 0),
                    stop=(g == GROUPS - 1),
                )

            def latent_passes(j, latent, groups):
                for g in groups:
                    first_pass(j, g, slice(0, LATENT), latent[:])

            def rope_passes(bank, tiles):
                for n, j in enumerate(tiles):
                    for g in range(GROUPS):
                        first_pass(j, g, slice(LATENT, A_COLS), bank[:, n * ROPE : (n + 1) * ROPE])

            def reciprocal_rms(latent):
                squares = norm.tile([P, LATENT], BF16)
                mean_sq = norm.tile([P, 1], F32)
                nc.scalar.activation(
                    out=squares[:], in_=latent[:], func=ACT.Square,
                    scale=1.0 / math.sqrt(LATENT), accum_out=mean_sq[:],
                )
                rstd = norm.tile([P, 1], F32)
                nc.scalar.activation(
                    out=rstd[:], in_=mean_sq[:], func=ACT.Abs_reciprocal_sqrt, bias=EPS, scale=1.0
                )
                return rstd

            def normalise(normed, latent, rstd, planes):
                nc.vector.scalar_tensor_tensor(
                    out=normed[:, planes, :],
                    in0=latent[:].rearrange("p (q t) -> p t q", t=PACK)[:, planes, :],
                    scalar=rstd[:, 0:1], in1=gain[:, planes, :], op0=ALU.mult, op1=ALU.mult,
                )

            def turn_h(turned, normed, planes):
                for i, t in enumerate(range(planes.start, planes.stop)):
                    nc.tensor.transpose(out=turned[:, i, :], in_=normed[:, t, :], identity=ident[:])

            def round_h(h_grouped, turned, planes, copy):
                copy(
                    out=h_grouped[:, :, planes],
                    in_=turned[:, 0 : planes.stop - planes.start, :].rearrange("p t k -> p k t"),
                )

            def quantise_h(h_grouped):
                codes = norm.tile([P, P], U32, align_bytes=64)
                scales = norm.tile([P, P], U8, align_bytes=64)
                nc.vector.quantize_mx(
                    out=codes[:].bitcast(FP8X4),
                    scales=scales[:],
                    in_=h_grouped[:].rearrange("p k t -> p (k t)"),
                )
                return codes, scales

            def rotate(bank, tiles):
                lo, count = tiles.start, len(tiles)
                prod = rope.tile([P, 2, EARLY * ROPE], F32)
                for c in range(2):
                    nc.vector.tensor_tensor(
                        out=prod[:, c, 0 : count * ROPE].rearrange("p (j r f) -> p j r f", j=count, f=HALF),
                        in0=bank[:, 0 : count * ROPE].rearrange("p (j r f) -> p j r f", j=count, f=HALF),
                        in1=tab[:, c, lo : lo + count, :].unsqueeze(2).to_broadcast([P, count, 2, HALF]),
                        op=ALU.mult,
                    )
                own = prod[:, 0, 0 : count * ROPE].rearrange("p (m e) -> p m e", e=2)
                carry = prod[:, 1, 0 : count * ROPE].rearrange("p (m e) -> p m e", e=2)
                rotated = rope.tile([P, EARLY * ROPE], F32)
                rotated_pairs = rotated[:, 0 : count * ROPE].rearrange("p (m e) -> p m e", e=2)
                for e in range(2):
                    nc.gpsimd.tensor_tensor(
                        out=rotated_pairs[:, :, e], in0=own[:, :, e], in1=carry[:, :, 1 - e], op=ALU.add
                    )
                return rotated

            def spread_rope(rotated, tiles, i):
                lo, count = tiles.start, len(tiles)
                nc.gpsimd.tensor_scalar(
                    out=k_sb[:, i, :, lo : lo + count, NOPE:K_OUT],
                    in0=rotated[:, 0 : count * ROPE].rearrange("p (j f) -> p j f", f=ROPE)
                    .unsqueeze(1).to_broadcast([P, 2, count, ROPE]),
                    scalar1=1.0, scalar2=0.0, op0=ALU.mult, op1=ALU.add,
                )

            k_sb = const.tile([P, HALF_HEADS, 2, TOK, K_OUT], F32)
            v_sb = const.tile([P, HALF_HEADS, 2, TOK, VDIM], F32)

            def second_matmul(m, e, h_mx_j, pool=kv_ps, tag="kv"):
                col = (m + UNITS * e) * PAIR_COLS
                plane, in_plane = col // B_PLANE_COLS, col % B_PLANE_COLS
                codes, scales = h_mx_j
                kv = pool.tile([P, 512], F32, tag=tag, name="kv")
                for lo, hi in ((0, 256), (256, PAIR_COLS)):
                    nc.tensor.matmul_mx(
                        out=kv[:, lo:hi],
                        lhsT=codes[:].bitcast(FP8X4),
                        lhsT_scale=scales[:],
                        rhs=wb_words[:, col + lo : col + hi].bitcast(FP8X4),
                        rhs_scale=wb_planes[4 * plane : P, in_plane + lo : in_plane + hi],
                        start=True,
                        stop=True,
                    )
                return kv

            def by_head(kv):
                return kv[:, 0:PAIR_COLS].rearrange("p (h c) -> p h c", h=PAIR)

            def copy_v(m, e, j, kv, copy):
                copy(
                    out=v_sb[:, PAIR * m : PAIR * (m + 1), e, j, :],
                    in_=by_head(kv)[:, :, NOPE:HEAD_COLS],
                )

            def copy_nope(m, e, j, kv, copy):
                copy(
                    out=k_sb[:, PAIR * m : PAIR * (m + 1), e, j, 0:NOPE],
                    in_=by_head(kv)[:, :, 0:NOPE],
                )

            def store_bank(out, rows, width, m, e, tiles):
                lo, hi = tiles.start * width, tiles.stop * width
                by_head = out.rearrange("b h (p j) d -> h p b (j d)", j=TOK)
                for i in range(PAIR * m, PAIR * (m + 1)):
                    nc.sync.dma_start(
                        out=by_head[i + HALF_HEADS * e][:, :, lo:hi],
                        in_=rows[:, i, e, :, :].rearrange("p j d -> p (j d)")[:, lo:hi],
                    )

            def store_unit(out, rows, width, m, tiles):
                lo, hi = tiles.start * width, tiles.stop * width
                by_i = out.rearrange("b (e i) (p j) d -> i p (b e) (j d)", e=2, j=TOK)
                for i in range(PAIR * m, PAIR * (m + 1)):
                    nc.sync.dma_start(
                        out=by_i[i][:, :, lo:hi],
                        in_=rows[:, i, :, :, :].rearrange("p e j d -> p e (j d)")[:, :, lo:hi],
                    )

            v_copy, s_copy = nc.vector.tensor_copy, nc.scalar.copy
            both = (v_copy, s_copy)
            early, late, every = range(0, EARLY), range(EARLY, TOK), range(0, TOK)

            def new_latent():
                latent = []
                for j in range(2):
                    latent_j = lat_ps.tile([P, LATENT], F32, name="latent_j")
                    latent.append(latent_j)
                return latent

            whole, halves = slice(0, PACK), (slice(0, PACK // 2), slice(PACK // 2, PACK))

            def new_normed():
                normed = norm.tile([P, PACK, P], F32)
                h_grouped = norm.tile([P, P, PACK], BF16, align_bytes=64)
                return normed, h_grouped

            def turn_first(normed):
                turned = tp_ps.tile([P, PACK, P], F32, tag="tp")
                turn_h(turned, normed, whole)
                return turned

            def norm_of_second(latent_j, rstd):
                normed, h_grouped = new_normed()
                for half, pool, tag in zip(halves, (tp_ps, kv_ps), ("tp", "kv")):
                    normalise(normed, latent_j, rstd, half)
                    turned = pool.tile([P, PACK, P], F32, tag=tag)
                    turn_h(turned, normed, half)
                    round_h(h_grouped, turned, half, s_copy)
                return h_grouped

            warm_bank = rope_ps.tile([P, 512], F32, tag="rope")
            keep_warm(zeros[:], WARM_START, warm_bank[:])
            xt = [turn_x(0, half, tp_ps, "tp") for half in range(2)]
            copy_x(0, 0, xt[0], v_copy)
            copy_x(0, 1, xt[1], s_copy)
            keep_warm(zeros[:], WARM_TURN[0], warm_bank[:])
            xt = [turn_x(1, half, kv_ps, "kv") for half in range(2)]
            keep_warm(zeros[:], WARM_TURN[1], warm_bank[:])
            quantise_x(0, 0)
            subtract_whole_turns()
            copy_x(1, 0, xt[0], s_copy)
            take_sines()
            quantise_x(0, 1)
            quantise_x(1, 0)
            copy_x(1, 1, xt[1], v_copy)
            nc.scalar.activation(
                out=warm[:, 1:2], in_=tab[:, 0, 0, 0:1], func=ACT.Abs_reciprocal_sqrt, bias=1.0, scale=0.0
            )
            quantise_x(1, 1)
            latent = new_latent()
            for j in early:
                latent_passes(j, latent[j], range(0, 2))
            latent_passes(0, latent[0], range(2, GROUPS))
            gain = const.tile([P, PACK, P], F32)
            gain_bank = kv_ps.tile([P, 512], F32, tag="kv")
            nc.tensor.matmul(out=gain_bank[:], lhsT=ones[:], rhs=gain_row[:], start=True, stop=True)
            v_copy(out=gain[:], in_=gain_bank[:].rearrange("p (q t) -> p t q", t=PACK))
            latent_passes(1, latent[1], range(2, GROUPS))
            x_bank_0 = turn_x(2, 0, kv_ps, "kv")
            warm_bank = kv_ps.tile([P, 512], F32, tag="kv")
            keep_warm(zeros[:], WARM_NORM, warm_bank[:])
            rstd_0 = reciprocal_rms(latent[0])
            normed_0, h_0 = new_normed()
            normalise(normed_0, latent[0], rstd_0, whole)
            rstd_1 = reciprocal_rms(latent[1])
            copy_x(2, 0, x_bank_0, s_copy)
            turned_0 = turn_first(normed_0)
            h_1 = norm_of_second(latent[1], rstd_1)
            r_bank = rope_ps.tile([P, 512], F32, tag="rope")
            rope_passes(r_bank, early)
            round_h(h_0, turned_0, whole, v_copy)
            h_mx = [quantise_h(h_0), quantise_h(h_1)]
            rotated = rotate(r_bank, early)
            for i in range(HALF_HEADS):
                spread_rope(rotated, early, i)

            def multiply(m, e, tiles):
                return [second_matmul(m, e, h_mx[j]) for j in tiles]

            def copy_vs(m, e, tiles, kv, copies):
                for j, kv_j, copy in zip(tiles, kv, copies):
                    copy_v(m, e, j, kv_j, copy)

            def copy_nopes(m, e, tiles, kv, copies):
                for j, kv_j, copy in zip(tiles, kv, copies):
                    copy_nope(m, e, j, kv_j, copy)

            def store_v_of_bank(m, e, tiles):
                store_bank(out_1, v_sb, VDIM, m, e, tiles)

            def store_k_of_bank(m, e, tiles):
                store_bank(out_0, k_sb, K_OUT, m, e, tiles)

            def store_v_of_unit(m, tiles):
                store_unit(out_1, v_sb, VDIM, m, tiles)

            def store_k_of_unit(m, tiles):
                store_unit(out_0, k_sb, K_OUT, m, tiles)

            def finish_early(m, e, kv, copies):
                copy_vs(m, e, early, kv, copies)
                store_v_of_bank(m, e, early)
                copy_nopes(m, e, early, kv, copies)
                store_k_of_bank(m, e, early)

            kv_0 = multiply(0, 0, early)
            kv_1 = [second_matmul(0, 1, h_mx[0]), second_matmul(0, 1, h_mx[1], lat_ps, "latent_j")]
            x_bank_1 = turn_x(2, 1, tp_ps, "tp")
            x_bank_2 = turn_x(3, 0, tp_ps, "tp")
            swapped = (s_copy, v_copy)
            copy_vs(0, 0, early, kv_0, swapped)
            store_v_of_bank(0, 0, early)
            copy_vs(0, 1, early, kv_1, swapped)
            store_v_of_bank(0, 1, early)
            copy_nopes(0, 0, early, kv_0, swapped)
            store_k_of_bank(0, 0, early)
            copy_nopes(0, 1, early, kv_1, swapped)
            store_k_of_bank(0, 1, early)
            kv = multiply(1, 0, early)
            quantise_x(2, 0)
            copy_x(2, 1, x_bank_1, s_copy)
            copy_x(3, 0, x_bank_2, v_copy)
            quantise_x(2, 1)
            x_bank_3 = turn_x(3, 1, tp_ps, "tp")
            quantise_x(3, 0)
            copy_x(3, 1, x_bank_3, v_copy)
            quantise_x(3, 1)
            latent = new_latent()
            latent_passes(2, latent[0], range(GROUPS))
            finish_early(1, 0, kv, (s_copy, s_copy))
            kv = multiply(1, 1, early)
            rstd_0 = reciprocal_rms(latent[0])
            latent_passes(3, latent[1], range(GROUPS))
            finish_early(1, 1, kv, both)
            kv = multiply(2, 0, early)
            normed_0, h_0 = new_normed()
            normalise(normed_0, latent[0], rstd_0, whole)
            rstd_1 = reciprocal_rms(latent[1])
            turned_0 = turn_first(normed_0)
            finish_early(2, 0, kv, (v_copy, v_copy))
            kv = multiply(2, 1, early)
            copy_v(2, 1, 0, kv[0], s_copy)
            copy_nope(2, 1, 0, kv[0], s_copy)
            h_1 = norm_of_second(latent[1], rstd_1)
            copy_v(2, 1, 1, kv[1], v_copy)
            store_v_of_bank(2, 1, early)
            copy_nope(2, 1, 1, kv[1], v_copy)
            store_k_of_bank(2, 1, early)
            round_h(h_0, turned_0, whole, v_copy)
            q_0 = quantise_h(h_0)
            r_bank = rope_ps.tile([P, 512], F32, tag="rope")
            rope_passes(r_bank, late)
            h_mx += [q_0, quantise_h(h_1)]

            def finish(m, e, tiles):
                kv = multiply(m, e, tiles)
                copy_vs(m, e, tiles, kv, both)
                copy_nopes(m, e, tiles, kv, both)

            rotated = rotate(r_bank, late)
            for i in range(HALF_HEADS):
                spread_rope(rotated, late, i)
            for m in range(UNITS - 1):
                for e in range(2):
                    copies = (s_copy, s_copy) if (m, e) == (0, 0) else both
                    kv = multiply(m, e, late)
                    copy_vs(m, e, late, kv, copies)
                    store_v_of_bank(m, e, late)
                    copy_nopes(m, e, late, kv, copies)
                store_k_of_unit(m, late)
            for tiles in (early, late):
                for e in range(2):
                    finish(UNITS - 1, e, tiles)
            store_v_of_unit(UNITS - 1, every)
            store_k_of_unit(UNITS - 1, every)
